import numpy as np
import ml_dtypes


def mxq(x, axis, fmt="e4m3"):
    dtype, down = {"e4m3": (ml_dtypes.float8_e4m3fn, 7), "e5m2": (ml_dtypes.float8_e5m2, 14)}[fmt]
    v = np.moveaxis(np.asarray(x, np.float32).astype(ml_dtypes.bfloat16).astype(np.float64), axis, -1)
    blocks = v.reshape(v.shape[:-1] + (-1, 32))
    amax = np.abs(blocks).max(-1, keepdims=True)
    byte = np.maximum(np.where(amax > 0, np.frexp(amax)[1] - 1 + 127, 0) - down, 1)
    scale = np.exp2(byte - 127.0)
    codes = (blocks / scale).astype(np.float32).astype(dtype).astype(np.float64)
    return np.moveaxis((codes * scale).reshape(v.shape), -1, axis)


WIDE = False


def mx_kscale(k):
    if not WIDE:
        return np.ones(k)
    levels = np.array([10, -10, 5, -5, 0])
    if k % 512:
        return np.exp2(np.random.permutation(np.resize(levels, k // 32))).repeat(32)
    a = np.empty((k // 512, 16))
    for p in range(k // 512):
        a[p, :8] = np.random.permutation(np.resize(levels, 8))
        for g in range(8):
            far = levels[np.abs(levels - a[p, g]) >= 10]
            a[p, g + 8] = far[np.random.randint(len(far))]
    return np.exp2(a.ravel()).repeat(32)


BF16 = ml_dtypes.bfloat16


def bf(x):
    return np.asarray(x, np.float32).astype(BF16)


def f64(x):
    return np.asarray(x).astype(np.float64)


B, S, D_MODEL, N_H, D_H, D_CQ, D_CKV, D_HR = 1, 512, 2048, 16, 128, 1024, 512, 128
ROPE_BASE = 10000.0


def rope_cos_sin(seq_len, dim):
    inv_freq = 1.0 / (ROPE_BASE ** (np.arange(0, dim, 2) / dim))
    ang = np.arange(seq_len)[:, None] * inv_freq[None, :]
    return np.cos(ang), np.sin(ang)


def rope(t, cos, sin):
    shp = t.shape
    d2 = shp[-1] // 2
    tr = t.reshape(shp[:-1] + (d2, 2))
    x0, x1 = tr[..., 0], tr[..., 1]
    bshape = (1, shp[1]) + (1,) * (x0.ndim - 3) + (d2,)
    cs, sn = cos.reshape(bshape), sin.reshape(bshape)
    return np.stack([x0 * cs - x1 * sn, x0 * sn + x1 * cs], axis=-1).reshape(shp)


def setup_inputs():
    s, t = mx_kscale(D_MODEL), mx_kscale(D_CQ)
    return {"h": bf(np.random.standard_normal((B, S, D_MODEL)) * s),
            "w_cq": bf(np.random.standard_normal((D_MODEL, D_CQ)) / np.sqrt(D_MODEL) / s[:, None] * t),
            "w_q": bf(np.random.standard_normal((D_CQ, N_H * D_H)) / np.sqrt(D_CQ) / t[:, None]),
            "w_qr": bf(np.random.standard_normal((D_CQ, N_H * D_HR)) / np.sqrt(D_CQ) / t[:, None])}


def reference(h, w_cq, w_q, w_qr):
    cos, sin = rope_cos_sin(S, D_HR)
    c_q = mxq(f64(h), 2, "e4m3") @ mxq(f64(w_cq), 0, "e4m3")
    cq = mxq(c_q, 2, "e4m3")
    q_c = (cq @ mxq(f64(w_q), 0, "e4m3")).reshape(B, S, N_H, D_H).transpose(0, 2, 1, 3)
    q_r = rope((cq @ mxq(f64(w_qr), 0, "e4m3")).reshape(B, S, N_H, D_HR), cos, sin).transpose(0, 2, 1, 3)
    return np.concatenate([q_c, q_r], axis=-1)

@@ -1,0 +1,356 @@
+import math
+from contextlib import ExitStack
+
+import concourse.mybir as mybir
+from concourse.masks import make_identity
+
+F32 = mybir.dt.float32
+BF16 = mybir.dt.bfloat16
+I32 = mybir.dt.int32
+U32 = mybir.dt.uint32
+U8 = mybir.dt.uint8
+FP8X4 = mybir.dt.float8_e4m3fn_x4
+ALU = mybir.AluOpType
+ACT = mybir.ActivationFunctionType
+
+P = 128
+PACK = 4
+K_PASS = P * PACK
+
+S = 512
+D_MODEL = 2048
+D_CQ = 1024
+HEADS = 16
+D_HEAD = 128
+PAIRS = D_HEAD // 2
+ROPE_BASE = 10000.0
+
+S_TILES = S // P
+PASSES_1 = D_MODEL // K_PASS
+PASSES_2 = D_CQ // K_PASS
+PIECE = 512
+LOAD_COLS = 2 * PIECE
+PARTS = LOAD_COLS // PIECE
+GROUP_HEADS = PIECE // D_HEAD
+HALVES = HEADS * D_HEAD // LOAD_COLS
+
+C_Q_BANKS = S_TILES * PASSES_2
+PIECES = 2 * PASSES_2 * HALVES * PARTS
+STEPS = S_TILES * HALVES * PARTS
+U_LAG = 4
+A_LAG = 8
+
+RAW_BUFS = 8
+VECTOR_COLS_BEFORE_ROPE = 256
+VECTOR_COLS_BESIDE_ROPE = 144
+
+ROUND_MAGIC = 1.5 * 2.0**23
+
+FLOPS = 2 * S * D_MODEL * D_CQ + 2 * S * D_CQ * 2 * HEADS * D_HEAD
+
+
+def rope_half_angles(nc, pool, for_even, for_odd):
+    shape = [P, S_TILES, PAIRS]
+    position_int = pool.tile([P, S_TILES], I32)
+    nc.gpsimd.iota(position_int[:], pattern=[[1, S_TILES]], base=0, channel_multiplier=S_TILES)
+    position = pool.tile([P, S_TILES], F32)
+    nc.vector.tensor_copy(out=position[:], in_=position_int[:])
+
+    frequency = pool.tile([P, PAIRS], F32)
+    nc.vector.memset(frequency[:, 0:1], 1.0)
+    filled = 1
+    while filled < PAIRS:
+        nc.vector.tensor_scalar_mul(
+            out=frequency[:, filled : 2 * filled],
+            in0=frequency[:, 0:filled],
+            scalar1=ROPE_BASE ** (-2.0 * filled / D_HEAD),
+        )
+        filled *= 2
+    turns = pool.tile(shape, F32)
+    nc.vector.scalar_tensor_tensor(
+        out=turns[:],
+        in0=frequency[:].unsqueeze(1).to_broadcast(shape),
+        scalar=1.0 / (2.0 * math.pi),
+        in1=position[:].unsqueeze(2).to_broadcast(shape),
+        op0=ALU.mult,
+        op1=ALU.mult,
+    )
+    whole_turns = pool.tile(shape, F32)
+    nc.vector.tensor_scalar(
+        out=whole_turns[:], in0=turns[:], scalar1=ROUND_MAGIC, scalar2=ROUND_MAGIC, op0=ALU.add, op1=ALU.subtract
+    )
+    nc.vector.tensor_tensor(out=turns[:], in0=turns[:], in1=whole_turns[:], op=ALU.subtract)
+
+    sin_half = pool.tile(shape, F32)
+    nc.scalar.activation(out=sin_half[:], in_=turns[:], func=ACT.Sin, scale=math.pi)
+    sin_quarter = pool.tile(shape, F32)
+    nc.scalar.activation(out=sin_quarter[:], in_=turns[:], func=ACT.Sin, scale=math.pi / 2.0)
+    square = pool.tile(shape, F32)
+    nc.scalar.activation(out=square[:], in_=sin_half[:], func=ACT.Square)
+    nc.scalar.activation(out=for_even[:, :, :, 0], in_=square[:], func=ACT.Copy, scale=-2.0, bias=1.0)
+    nc.scalar.activation(out=for_odd[:, :, :, 1], in_=square[:], func=ACT.Copy, scale=-2.0, bias=1.0)
+    cos_half = pool.tile(shape, F32)
+    nc.scalar.activation(out=cos_half[:], in_=sin_quarter[:], func=ACT.Square)
+    nc.scalar.activation(out=cos_half[:], in_=cos_half[:], func=ACT.Copy, scale=-2.0, bias=1.0)
+    return sin_half, cos_half
+
+
+def quantise(nc, operand, grouped):
+    nc.vector.quantize_mx(out=operand[0][:].bitcast(FP8X4), scales=operand[1][:], in_=grouped)
+
+
+def mx_operand(pool, width, label):
+    codes = pool.tile([P, width], U32, align_bytes=64, name=label + "_codes")
+    scales = pool.tile([P, width], U8, align_bytes=64, name=label + "_scales")
+    return codes, scales
+
+
+def columns(operand, start, width):
+    return operand[0][:, start : start + width], operand[1][:, start : start + width]
+
+
+def multiply_mx(nc, acc, stationary, moving, first, last):
+    nc.tensor.matmul_mx(
+        out=acc,
+        lhsT=stationary[0].bitcast(FP8X4),
+        lhsT_scale=stationary[1],
+        rhs=moving[0].bitcast(FP8X4),
+        rhs_scale=moving[1],
+        start=first,
+        stop=last,
+    )
+
+
+def regroup(nc, grouped, raw_piece, vector_cols):
+    nc.vector.tensor_copy(
+        out=grouped[:, :vector_cols, :].rearrange("p (w i) t -> p w t i", i=4),
+        in_=raw_piece[:, :, :vector_cols].rearrange("p t (w i) -> p w t i", i=4),
+    )
+    nc.scalar.copy(
+        out=grouped[:, vector_cols:, :].rearrange("p (w i) t -> p w t i", i=4),
+        in_=raw_piece[:, :, vector_cols:].rearrange("p t (w i) -> p w t i", i=4),
+    )
+
+
+def regroup_permuted(nc, grouped, raw_piece, vector_cols):
+    split = vector_cols // PACK
+    dst = grouped[:].rearrange("p (t m) j -> p m j t", t=PACK)
+    src = raw_piece.rearrange("p j (m t) -> p m j t", t=PACK)
+    nc.vector.tensor_copy(out=dst[:, :split], in_=src[:, :split])
+    nc.scalar.copy(out=dst[:, split:], in_=src[:, split:])
+
+
+def tile_mla_pa_kernel(tc, h, w_cq, w_q, w_qr, out):
+    nc = tc.nc
+    with ExitStack() as ctx:
+        ctx.enter_context(tc.manual_schedule())
+        const = ctx.enter_context(tc.tile_pool(name="const", bufs=1))
+        keep = ctx.enter_context(tc.tile_pool(name="keep", bufs=1))
+        raw_pool = ctx.enter_context(tc.tile_pool(name="raw_pool", bufs=RAW_BUFS))
+        stage = ctx.enter_context(tc.tile_pool(name="stage", bufs=4))
+        c_q_stage = ctx.enter_context(tc.tile_pool(name="c_q_stage", bufs=2))
+        psum_u = ctx.enter_context(tc.psum_pool(name="psum_u", bufs=4))
+        psum_a = ctx.enter_context(tc.psum_pool(name="psum_a", bufs=2))
+        psum_c_q = ctx.enter_context(tc.psum_pool(name="psum_c_q", bufs=2))
+
+        identity = const.tile([P, P], F32)
+        make_identity(nc, identity[:])
+        for_even = const.tile([P, S_TILES, PAIRS, 2], F32)
+        for_odd = const.tile([P, S_TILES, PAIRS, 2], F32)
+        sin_half, cos_half = rope_half_angles(nc, const, for_even, for_odd)
+
+        h_rows = h.flatten_outer_dims().rearrange("(p a) k -> p a k", a=S_TILES)
+        h_mx = []
+        with tc.tile_pool(name="h_pool", bufs=S_TILES) as h_pool, tc.tile_pool(name="h_stage", bufs=2) as h_stage:
+            h_raw = []
+            for a in range(S_TILES):
+                h_tile = h_pool.tile([P, D_MODEL], BF16)
+                nc.sync.dma_start(out=h_tile[:], in_=h_rows[:, a, :])
+                h_raw.append(h_tile)
+
+            w_cq_rows = w_cq.rearrange("(c p t) n -> c p t n", c=PASSES_1, t=PACK)
+            sources = [w_cq_rows[c] for c in range(PASSES_1)]
+            for half in range(HALVES):
+                for weight in (w_qr, w_q):
+                    rows = weight.rearrange("(g p t) n -> g p t n", g=PASSES_2, t=PACK)
+                    for g in range(PASSES_2):
+                        sources.append(rows[g][:, :, half * LOAD_COLS : (half + 1) * LOAD_COLS])
+            raw_tiles = []
+
+            def load_next_weights():
+                if len(raw_tiles) < len(sources):
+                    source = sources[len(raw_tiles)]
+                    raw = raw_pool.tile([P, PACK, LOAD_COLS], BF16)
+                    nc.sync.dma_start(out=raw[:], in_=source)
+                    raw_tiles.append(raw)
+
+            for j in range(RAW_BUFS):
+                load_next_weights()
+
+            for a in range(S_TILES):
+                h_words = h_raw[a][:].bitcast(F32)
+                h_grouped = h_stage.tile([P, PASSES_1, P, PACK], BF16, align_bytes=64)
+                for b in range(PASSES_1 // 2):
+                    flipped = psum_u.tile([P, 4, P], F32, tag="u_bank")
+                    for j in range(4):
+                        c, u = divmod(4 * b + j, 2)
+                        words = h_words[:, 2 * P * c + u : 2 * P * (c + 1) : 2]
+                        nc.tensor.transpose(flipped[:, j, :], words, identity[:])
+                    nc.scalar.copy(
+                        out=h_grouped[:, 2 * b : 2 * b + 2].bitcast(F32),
+                        in_=flipped[:].rearrange("q (c u) s -> q c s u", u=2),
+                    )
+                h_mx.append(mx_operand(keep, PASSES_1 * P, "h%d" % a))
+                quantise(nc, h_mx[a], h_grouped[:].rearrange("q c s t -> q (c s t)"))
+        rope_pool = ctx.enter_context(tc.tile_pool(name="rope_pool", bufs=4, reuse_waits="tile"))
+        result_pool = ctx.enter_context(tc.tile_pool(name="result_pool", bufs=5, reuse_waits="tile"))
+
+        sin_x = const.tile([P, S_TILES, PAIRS], F32)
+        nc.vector.scalar_tensor_tensor(
+            out=sin_x[:], in0=sin_half[:], scalar=2.0, in1=cos_half[:], op0=ALU.mult, op1=ALU.mult
+        )
+        nc.scalar.copy(out=for_even[:, :, :, 1], in_=sin_x[:])
+        nc.scalar.mul(out=for_odd[:, :, :, 0], in_=sin_x[:], mul=-1.0)
+
+        def regroup_piece(raw, part, vector_cols, label, regroup_columns=regroup):
+            grouped = stage.tile([P, PIECE, PACK], BF16, align_bytes=64)
+            regroup_columns(nc, grouped, raw[:, :, part * PIECE : (part + 1) * PIECE], vector_cols)
+            return grouped, mx_operand(keep, PIECE, label)
+
+        def quantise_piece(piece):
+            grouped, operand = piece
+            quantise(nc, operand, grouped[:].rearrange("p w t -> p (w t)"))
+
+        w_cq_mx = []
+        waiting = None
+        for c in range(PASSES_1):
+            w_cq_mx.append([])
+            for g in range(PASSES_2):
+                piece = regroup_piece(raw_tiles[c], g, VECTOR_COLS_BEFORE_ROPE, "w_cq%d%d" % (c, g), regroup_permuted)
+                w_cq_mx[c].append(piece[1])
+                if waiting is not None:
+                    quantise_piece(waiting)
+                waiting = piece
+            load_next_weights()
+        quantise_piece(waiting)
+        waiting = None
+
+        c_q_grouped = {}
+        c_q_mx = {}
+        w_mx = {}
+        products = {}
+        results = {}
+        out_rows = out.rearrange("b n (p a) d -> p (b n) a d", a=S_TILES)
+
+        def step_of(j):
+            half, rest = divmod(j, S_TILES * PARTS)
+            a, part = divmod(rest, PARTS)
+            return half, part, a
+
+        def c_q_bank(b):
+            a, g = divmod(b, PASSES_2)
+            bank = psum_c_q.tile([P, PACK, P], F32)
+            for t in range(PACK):
+                for c in range(PASSES_1):
+                    multiply_mx(
+                        nc,
+                        bank[:, t, :],
+                        columns(w_cq_mx[c][g], t * P, P),
+                        columns(h_mx[a], c * P, P),
+                        first=(c == 0),
+                        last=(c == PASSES_1 - 1),
+                    )
+            return bank
+
+        def copy_c_q_bank(b, bank):
+            a, g = divmod(b, PASSES_2)
+            if g == 0:
+                c_q_grouped[a] = c_q_stage.tile([P, PASSES_2, P, PACK], BF16, align_bytes=64, name="c_q_grouped")
+            nc.scalar.copy(out=c_q_grouped[a][:, g], in_=bank[:].rearrange("m t s -> m s t"))
+
+        def quantise_c_q(a):
+            c_q_mx[a] = mx_operand(keep, PASSES_2 * P, "c_q%d" % a)
+            quantise(nc, c_q_mx[a], c_q_grouped[a][:].rearrange("m g s t -> m (g s t)"))
+
+        def multiply_by_weights(j, weight, pool):
+            half, part, a = step_of(j)
+            bank = pool.tile([P, GROUP_HEADS, D_HEAD], F32, name="bank%d" % weight, tag="u_bank" if weight == 0 else "a_bank")
+            for g in range(PASSES_2):
+                multiply_mx(
+                    nc,
+                    bank[:].rearrange("p n d -> p (n d)"),
+                    columns(c_q_mx[a], g * P, P),
+                    columns(w_mx[(weight, half, part, g)], 0, PIECE),
+                    first=(g == 0),
+                    last=(g == PASSES_2 - 1),
+                )
+            return bank
+
+        def rope_products(j, u_bank):
+            a = step_of(j)[2]
+            whole = [P, GROUP_HEADS, PAIRS, 2]
+            u_pairs = u_bank[:].rearrange("p n (i e) -> p n i e", e=2)
+            from_even = rope_pool.tile(whole, F32)
+            nc.vector.tensor_tensor(
+                out=from_even[:],
+                in0=u_pairs[:, :, :, 0:1].to_broadcast(whole),
+                in1=for_even[:, a].unsqueeze(1).to_broadcast(whole),
+                op=ALU.mult,
+            )
+            from_odd = rope_pool.tile(whole, F32)
+            nc.vector.tensor_tensor(
+                out=from_odd[:],
+                in0=u_pairs[:, :, :, 1:2].to_broadcast(whole),
+                in1=for_odd[:, a].unsqueeze(1).to_broadcast(whole),
+                op=ALU.mult,
+            )
+            products[j] = (from_even, from_odd)
+
+        def rope_sum(j):
+            from_even, from_odd = products[j]
+            results[j] = result_pool.tile([P, GROUP_HEADS, 2 * D_HEAD], F32, name="result")
+            nc.gpsimd.tensor_tensor(
+                out=results[j][:, :, D_HEAD:],
+                in0=from_even[:].rearrange("p n i e -> p n (i e)"),
+                in1=from_odd[:].rearrange("p n i e -> p n (i e)"),
+                op=ALU.add,
+            )
+
+        def store(j):
+            half, part, a = step_of(j)
+            first_head = (half * PARTS + part) * GROUP_HEADS
+            nc.sync.dma_start(out=out_rows[:, first_head : first_head + GROUP_HEADS, a, :], in_=results[j][:])
+
+        for i in range(STEPS + A_LAG):
+            u_step, a_step = i - U_LAG, i - A_LAG
+            if i < C_Q_BANKS:
+                new_c_q = c_q_bank(i)
+            if 0 <= u_step < STEPS:
+                u_bank = multiply_by_weights(u_step, 0, psum_u)
+            if 0 <= a_step:
+                a_bank = multiply_by_weights(a_step, 1, psum_a)
+            piece = None
+            if i < PIECES:
+                load, part = divmod(i, PARTS)
+                half, rest = divmod(load, 2 * PASSES_2)
+                weight, g = divmod(rest, PASSES_2)
+                piece = regroup_piece(
+                    raw_tiles[PASSES_1 + load],
+                    part,
+                    VECTOR_COLS_BEFORE_ROPE if i < U_LAG else VECTOR_COLS_BESIDE_ROPE,
+                    "w%d%d%d%d" % (weight, half, part, g),
+                )
+                w_mx[(weight, half, part, g)] = piece[1]
+            if waiting is not None:
+                quantise_piece(waiting)
+            waiting = piece
+            if i < C_Q_BANKS:
+                copy_c_q_bank(i, new_c_q)
+            if 0 < i <= C_Q_BANKS and i % PASSES_2 == 0:
+                quantise_c_q(i // PASSES_2 - 1)
+            if 0 <= u_step < STEPS:
+                rope_products(u_step, u_bank)
+                rope_sum(u_step)
+            if 0 <= a_step:
+                nc.scalar.copy(out=results[a_step][:, :, 0:D_HEAD], in_=a_bank[:])
+                store(a_step)

@@ -6,7 +6,6 @@ from concourse.masks import make_identity
 
 F32 = mybir.dt.float32
 BF16 = mybir.dt.bfloat16
-I32 = mybir.dt.int32
 U32 = mybir.dt.uint32
 U8 = mybir.dt.uint8
 FP8X4 = mybir.dt.float8_e4m3fn_x4
@@ -34,65 +33,33 @@ PARTS = LOAD_COLS // PIECE
 GROUP_HEADS = PIECE // D_HEAD
 HALVES = HEADS * D_HEAD // LOAD_COLS
 
-C_Q_BANKS = S_TILES * PASSES_2
-PIECES = 2 * PASSES_2 * HALVES * PARTS
+CQ_PIECES = PASSES_2 * PASSES_1
+C_Q_BANKS = PASSES_2 * S_TILES
+W_PIECES = 2 * PASSES_2 * HALVES * PARTS
 STEPS = S_TILES * HALVES * PARTS
-U_LAG = 4
-A_LAG = 8
 
-RAW_BUFS = 8
-VECTOR_COLS_BEFORE_ROPE = 256
-VECTOR_COLS_BESIDE_ROPE = 144
+C_Q_START = PASSES_1 + 1
+U_START = CQ_PIECES + 4
+A_START = U_START + 4
+
+PSUM_MAIN = 6
+RAW_BUFS = 6
+UNIT = 4
+UNITS = PIECE // UNIT
+BANK_UNITS = 64
+
+
+def shares(n):
+    if n < PASSES_1:
+        return 32, 32
+    if n < CQ_PIECES + 3:
+        return 80, UNITS
+    return 20, BANK_UNITS
+
 
 ROUND_MAGIC = 1.5 * 2.0**23
 
 FLOPS = 2 * S * D_MODEL * D_CQ + 2 * S * D_CQ * 2 * HEADS * D_HEAD
-
-
-def rope_half_angles(nc, pool, for_even, for_odd):
-    shape = [P, S_TILES, PAIRS]
-    position_int = pool.tile([P, S_TILES], I32)
-    nc.gpsimd.iota(position_int[:], pattern=[[1, S_TILES]], base=0, channel_multiplier=S_TILES)
-    position = pool.tile([P, S_TILES], F32)
-    nc.vector.tensor_copy(out=position[:], in_=position_int[:])
-
-    frequency = pool.tile([P, PAIRS], F32)
-    nc.vector.memset(frequency[:, 0:1], 1.0)
-    filled = 1
-    while filled < PAIRS:
-        nc.vector.tensor_scalar_mul(
-            out=frequency[:, filled : 2 * filled],
-            in0=frequency[:, 0:filled],
-            scalar1=ROPE_BASE ** (-2.0 * filled / D_HEAD),
-        )
-        filled *= 2
-    turns = pool.tile(shape, F32)
-    nc.vector.scalar_tensor_tensor(
-        out=turns[:],
-        in0=frequency[:].unsqueeze(1).to_broadcast(shape),
-        scalar=1.0 / (2.0 * math.pi),
-        in1=position[:].unsqueeze(2).to_broadcast(shape),
-        op0=ALU.mult,
-        op1=ALU.mult,
-    )
-    whole_turns = pool.tile(shape, F32)
-    nc.vector.tensor_scalar(
-        out=whole_turns[:], in0=turns[:], scalar1=ROUND_MAGIC, scalar2=ROUND_MAGIC, op0=ALU.add, op1=ALU.subtract
-    )
-    nc.vector.tensor_tensor(out=turns[:], in0=turns[:], in1=whole_turns[:], op=ALU.subtract)
-
-    sin_half = pool.tile(shape, F32)
-    nc.scalar.activation(out=sin_half[:], in_=turns[:], func=ACT.Sin, scale=math.pi)
-    sin_quarter = pool.tile(shape, F32)
-    nc.scalar.activation(out=sin_quarter[:], in_=turns[:], func=ACT.Sin, scale=math.pi / 2.0)
-    square = pool.tile(shape, F32)
-    nc.scalar.activation(out=square[:], in_=sin_half[:], func=ACT.Square)
-    nc.scalar.activation(out=for_even[:, :, :, 0], in_=square[:], func=ACT.Copy, scale=-2.0, bias=1.0)
-    nc.scalar.activation(out=for_odd[:, :, :, 1], in_=square[:], func=ACT.Copy, scale=-2.0, bias=1.0)
-    cos_half = pool.tile(shape, F32)
-    nc.scalar.activation(out=cos_half[:], in_=sin_quarter[:], func=ACT.Square)
-    nc.scalar.activation(out=cos_half[:], in_=cos_half[:], func=ACT.Copy, scale=-2.0, bias=1.0)
-    return sin_half, cos_half
 
 
 def quantise(nc, operand, grouped):
@@ -121,141 +88,238 @@ def multiply_mx(nc, acc, stationary, moving, first, last):
     )
 
 
-def regroup(nc, grouped, raw_piece, vector_cols):
-    nc.vector.tensor_copy(
-        out=grouped[:, :vector_cols, :].rearrange("p (w i) t -> p w t i", i=4),
-        in_=raw_piece[:, :, :vector_cols].rearrange("p t (w i) -> p w t i", i=4),
-    )
-    nc.scalar.copy(
-        out=grouped[:, vector_cols:, :].rearrange("p (w i) t -> p w t i", i=4),
-        in_=raw_piece[:, :, vector_cols:].rearrange("p t (w i) -> p w t i", i=4),
-    )
-
-
-def regroup_permuted(nc, grouped, raw_piece, vector_cols):
-    split = vector_cols // PACK
-    dst = grouped[:].rearrange("p (t m) j -> p m j t", t=PACK)
-    src = raw_piece.rearrange("p j (m t) -> p m j t", t=PACK)
-    nc.vector.tensor_copy(out=dst[:, :split], in_=src[:, :split])
-    nc.scalar.copy(out=dst[:, split:], in_=src[:, split:])
-
-
 def tile_mla_pa_kernel(tc, h, w_cq, w_q, w_qr, out):
     nc = tc.nc
     with ExitStack() as ctx:
         ctx.enter_context(tc.manual_schedule())
         const = ctx.enter_context(tc.tile_pool(name="const", bufs=1))
         keep = ctx.enter_context(tc.tile_pool(name="keep", bufs=1))
+        cq_raw_pool = ctx.enter_context(tc.tile_pool(name="cq_raw_pool", bufs=CQ_PIECES))
         raw_pool = ctx.enter_context(tc.tile_pool(name="raw_pool", bufs=RAW_BUFS))
         stage = ctx.enter_context(tc.tile_pool(name="stage", bufs=4))
-        c_q_stage = ctx.enter_context(tc.tile_pool(name="c_q_stage", bufs=2))
-        psum_u = ctx.enter_context(tc.psum_pool(name="psum_u", bufs=4))
-        psum_a = ctx.enter_context(tc.psum_pool(name="psum_a", bufs=2))
-        psum_c_q = ctx.enter_context(tc.psum_pool(name="psum_c_q", bufs=2))
+        c_q_stage = ctx.enter_context(tc.tile_pool(name="c_q_stage", bufs=S_TILES))
+        psum_main = ctx.enter_context(tc.psum_pool(name="psum_main", bufs=PSUM_MAIN))
+        psum_a = ctx.enter_context(tc.psum_pool(name="psum_a", bufs=8 - PSUM_MAIN))
 
-        identity = const.tile([P, P], F32)
-        make_identity(nc, identity[:])
-        for_even = const.tile([P, S_TILES, PAIRS, 2], F32)
-        for_odd = const.tile([P, S_TILES, PAIRS, 2], F32)
-        sin_half, cos_half = rope_half_angles(nc, const, for_even, for_odd)
+        w_cq_rows = w_cq.rearrange("(c p t) n -> c p t n", c=PASSES_1, t=PACK)
+        cq_raw = []
+
+        def load_w_cq():
+            g, c = divmod(len(cq_raw), PASSES_1)
+            raw = cq_raw_pool.tile([P, PACK, PIECE], BF16, name="cq_raw")
+            nc.sync.dma_start(out=raw[:], in_=w_cq_rows[c][:, :, g * PIECE : (g + 1) * PIECE])
+            cq_raw.append(raw)
 
         h_rows = h.flatten_outer_dims().rearrange("(p a) k -> p a k", a=S_TILES)
         h_mx = []
-        with tc.tile_pool(name="h_pool", bufs=S_TILES) as h_pool, tc.tile_pool(name="h_stage", bufs=2) as h_stage:
+        w_sources = []
+        for half in range(HALVES):
+            for weight in (w_qr, w_q):
+                rows = weight.rearrange("(g p t) n -> g p t n", g=PASSES_2, t=PACK)
+                for g in range(PASSES_2):
+                    w_sources.append(rows[g][:, :, half * LOAD_COLS : (half + 1) * LOAD_COLS])
+        w_raw = []
+
+        def load_w():
+            raw = raw_pool.tile([P, PACK, LOAD_COLS], BF16, name="w_raw")
+            nc.sync.dma_start(out=raw[:], in_=w_sources[len(w_raw)])
+            w_raw.append(raw)
+
+        zero = const.tile([P, 1], F32)
+        nc.gpsimd.memset(zero[:], 0.0)
+        sin_zero = const.tile([P, 1], F32)
+        nc.scalar.activation(out=sin_zero[:], in_=zero[:], func=ACT.Sin)
+
+        shape = [P, S_TILES, PAIRS]
+        position = const.tile([P, S_TILES], F32)
+        nc.gpsimd.iota(
+            position[:],
+            pattern=[[1, S_TILES]],
+            base=0,
+            channel_multiplier=S_TILES,
+            allow_small_or_imprecise_dtypes=True,
+        )
+        identity = const.tile([P, P], F32)
+        make_identity(nc, identity[:])
+        identity_bf16 = const.tile([P, P], BF16)
+        nc.gpsimd.tensor_copy(out=identity_bf16[:], in_=identity[:])
+        nc.vector.tensor_scalar_mul(out=position[:], in0=position[:], scalar1=1.0 / (2.0 * math.pi))
+        frequency = const.tile([P, PAIRS], F32)
+        nc.vector.memset(frequency[:, 0:1], 1.0)
+        filled = 1
+        while filled < PAIRS:
+            nc.vector.tensor_scalar_mul(
+                out=frequency[:, filled : 2 * filled],
+                in0=frequency[:, 0:filled],
+                scalar1=ROPE_BASE ** (-2.0 * filled / D_HEAD),
+            )
+            filled *= 2
+        turns = const.tile(shape, F32)
+        nc.vector.tensor_tensor(
+            out=turns[:],
+            in0=frequency[:].unsqueeze(1).to_broadcast(shape),
+            in1=position[:].unsqueeze(2).to_broadcast(shape),
+            op=ALU.mult,
+        )
+        factors = const.tile([P, 3, S_TILES, PAIRS], F32)
+        for_even = factors[:, 1:3]
+        for_odd = factors[:, 0:2]
+        whole_turns = const.tile(shape, F32)
+        sin_half = const.tile(shape, F32)
+        sin_quarter = const.tile(shape, F32)
+        square = const.tile(shape, F32)
+        cos_half = const.tile(shape, F32)
+
+        nc.vector.tensor_scalar(
+            out=whole_turns[:], in0=turns[:], scalar1=ROUND_MAGIC, scalar2=ROUND_MAGIC, op0=ALU.add, op1=ALU.subtract
+        )
+        nc.vector.tensor_tensor(out=turns[:], in0=turns[:], in1=whole_turns[:], op=ALU.subtract)
+        nc.scalar.activation(out=sin_half[:], in_=turns[:], func=ACT.Sin, scale=math.pi)
+        nc.scalar.activation(out=sin_quarter[:], in_=turns[:], func=ACT.Sin, scale=math.pi / 2.0)
+        for sine, cosine in ((sin_half[:], factors[:, 1]), (sin_quarter[:], cos_half[:])):
+            nc.gpsimd.tensor_tensor(out=square[:], in0=sine, in1=sine, op=ALU.mult)
+            nc.gpsimd.tensor_scalar(out=cosine, in0=square[:], scalar1=-2.0, scalar2=1.0, op0=ALU.mult, op1=ALU.add)
+        nc.gpsimd.tensor_tensor(out=square[:], in0=sin_half[:], in1=cos_half[:], op=ALU.mult)
+        for sign, plane in ((2.0, 2), (-2.0, 0)):
+            nc.gpsimd.tensor_scalar(out=factors[:, plane], in0=square[:], scalar1=sign, scalar2=0.0, op0=ALU.mult, op1=ALU.add)
+
+        pieces = []
+        w_cq_mx = {}
+        w_mx = {}
+
+        grouped_tiles = {}
+        passed = {}
+
+        def views(n):
+            grouped = grouped_tiles[n]
+            if n < CQ_PIECES:
+                src = cq_raw[n][:].rearrange("p j (m t) -> p m j t", t=UNIT)
+                return src, grouped[:].rearrange("p (t m) j -> p m j t", t=UNIT)
+            load, part = divmod(n - CQ_PIECES, PARTS)
+            src = w_raw[load][:, :, part * PIECE : (part + 1) * PIECE].rearrange("p j (m t) -> p m j t", t=UNIT)
+            return src, grouped[:].rearrange("p (m t) j -> p m j t", t=UNIT)
+
+        def pass_through(n):
+            grouped_tiles[n] = stage.tile([P, PIECE, PACK], BF16, align_bytes=64, name="grouped")
+            src, dst = views(n)
+            passed[n] = []
+            first = shares(n)[1]
+            while first < UNITS:
+                width = min(BANK_UNITS, UNITS - first)
+                bank = psum_main.tile([P, width * UNIT * PACK], BF16, tag="bank", name="passed")
+                here = src[:, first : first + width]
+                if n < CQ_PIECES:
+                    here = here.rearrange("p m j t -> p t m j")
+                    to = grouped_tiles[n][:].rearrange("p (t m) j -> p t (m j)", t=UNIT)
+                    to = to[:, :, first * PACK : (first + width) * PACK]
+                    runs = UNIT * width * UNIT * PACK // (UNIT * 512)
+                    per = UNIT // runs
+                    moving = [here[:, r * per : (r + 1) * per] for r in range(runs)]
+                else:
+                    to = grouped_tiles[n][:].rearrange("p c j -> p (c j)")
+                    to = to[:, first * UNIT * PACK : (first + width) * UNIT * PACK]
+                    runs = width * UNIT * PACK // 512
+                    load, part = divmod(n - CQ_PIECES, PARTS)
+                    start = part * PIECE + first * UNIT
+                    cols = w_raw[load][:, :, start : start + width * UNIT].rearrange("p j c -> p c j")
+                    per = width * UNIT // runs
+                    moving = [cols[:, r * per : (r + 1) * per] for r in range(runs)]
+                for r in range(runs):
+                    nc.tensor.matmul(
+                        bank[:, r * 512 : (r + 1) * 512], lhsT=identity_bf16[:], rhs=moving[r], start=True, stop=True
+                    )
+                words = bank[:].bitcast(F32)
+                if n < CQ_PIECES:
+                    words = words.rearrange("p (t w) -> p t w", t=UNIT)
+                passed[n].append((words, to.bitcast(F32)))
+                first += width
+
+        def regroup(n):
+            src, dst = views(n)
+            for words, to in passed[n]:
+                nc.scalar.copy(out=to, in_=words)
+            v, sc = shares(n)
+            nc.vector.tensor_copy(out=dst[:, :v], in_=src[:, :v])
+            if sc > v:
+                nc.scalar.copy(out=dst[:, v:sc], in_=src[:, v:sc])
+            if n < CQ_PIECES:
+                operand = mx_operand(keep, PIECE, "w_cq%d" % n)
+                w_cq_mx[divmod(n, PASSES_1)] = operand
+            else:
+                load, part = divmod(n - CQ_PIECES, PARTS)
+                half, rest = divmod(load, 2 * PASSES_2)
+                weight, g = divmod(rest, PASSES_2)
+                operand = mx_operand(keep, PIECE, "w%d%d%d%d" % (weight, half, part, g))
+                w_mx[(weight, half, part, g)] = operand
+            pieces.append((grouped_tiles[n], operand))
+
+        def quantise_piece(n):
+            grouped, operand = pieces[n]
+            quantise(nc, operand, grouped[:].rearrange("p w t -> p (w t)"))
+
+        with tc.tile_pool(name="h_pool", bufs=S_TILES) as h_pool, tc.tile_pool(name="h_stage", bufs=S_TILES) as h_stage:
+            load_w_cq()
+            load_w_cq()
             h_raw = []
             for a in range(S_TILES):
                 h_tile = h_pool.tile([P, D_MODEL], BF16)
                 nc.sync.dma_start(out=h_tile[:], in_=h_rows[:, a, :])
                 h_raw.append(h_tile)
-
-            w_cq_rows = w_cq.rearrange("(c p t) n -> c p t n", c=PASSES_1, t=PACK)
-            sources = [w_cq_rows[c] for c in range(PASSES_1)]
-            for half in range(HALVES):
-                for weight in (w_qr, w_q):
-                    rows = weight.rearrange("(g p t) n -> g p t n", g=PASSES_2, t=PACK)
-                    for g in range(PASSES_2):
-                        sources.append(rows[g][:, :, half * LOAD_COLS : (half + 1) * LOAD_COLS])
-            raw_tiles = []
-
-            def load_next_weights():
-                if len(raw_tiles) < len(sources):
-                    source = sources[len(raw_tiles)]
-                    raw = raw_pool.tile([P, PACK, LOAD_COLS], BF16)
-                    nc.sync.dma_start(out=raw[:], in_=source)
-                    raw_tiles.append(raw)
-
+            while len(cq_raw) < CQ_PIECES:
+                load_w_cq()
             for j in range(RAW_BUFS):
-                load_next_weights()
+                load_w()
 
+            pass_through(0)
+            pass_through(1)
+            regroup(0)
+            regroup(1)
+            quantise_piece(0)
+            h_grouped = []
             for a in range(S_TILES):
                 h_words = h_raw[a][:].bitcast(F32)
-                h_grouped = h_stage.tile([P, PASSES_1, P, PACK], BF16, align_bytes=64)
+                grouped_a = h_stage.tile([P, PASSES_1, P, PACK], BF16, align_bytes=64)
+                h_grouped.append(grouped_a)
                 for b in range(PASSES_1 // 2):
-                    flipped = psum_u.tile([P, 4, P], F32, tag="u_bank")
+                    flipped = psum_main.tile([P, 4, P], F32, tag="bank")
                     for j in range(4):
                         c, u = divmod(4 * b + j, 2)
                         words = h_words[:, 2 * P * c + u : 2 * P * (c + 1) : 2]
                         nc.tensor.transpose(flipped[:, j, :], words, identity[:])
-                    nc.scalar.copy(
-                        out=h_grouped[:, 2 * b : 2 * b + 2].bitcast(F32),
-                        in_=flipped[:].rearrange("q (c u) s -> q c s u", u=2),
-                    )
+                    target = grouped_a[:, 2 * b : 2 * b + 2].bitcast(F32)
+                    flipped_words = flipped[:].rearrange("q (c u) s -> q c s u", u=2)
+                    if b == 0:
+                        nc.scalar.copy(out=target, in_=flipped_words)
+                    else:
+                        nc.vector.tensor_copy(out=target, in_=flipped_words)
                 h_mx.append(mx_operand(keep, PASSES_1 * P, "h%d" % a))
-                quantise(nc, h_mx[a], h_grouped[:].rearrange("q c s t -> q (c s t)"))
+                if a == 0:
+                    quantise_piece(1)
+                else:
+                    quantise(nc, h_mx[a - 1], h_grouped[a - 1][:].rearrange("q c s t -> q (c s t)"))
+            quantise(nc, h_mx[-1], h_grouped[-1][:].rearrange("q c s t -> q (c s t)"))
         rope_pool = ctx.enter_context(tc.tile_pool(name="rope_pool", bufs=4, reuse_waits="tile"))
-        result_pool = ctx.enter_context(tc.tile_pool(name="result_pool", bufs=5, reuse_waits="tile"))
-
-        sin_x = const.tile([P, S_TILES, PAIRS], F32)
-        nc.vector.scalar_tensor_tensor(
-            out=sin_x[:], in0=sin_half[:], scalar=2.0, in1=cos_half[:], op0=ALU.mult, op1=ALU.mult
-        )
-        nc.scalar.copy(out=for_even[:, :, :, 1], in_=sin_x[:])
-        nc.scalar.mul(out=for_odd[:, :, :, 0], in_=sin_x[:], mul=-1.0)
-
-        def regroup_piece(raw, part, vector_cols, label, regroup_columns=regroup):
-            grouped = stage.tile([P, PIECE, PACK], BF16, align_bytes=64)
-            regroup_columns(nc, grouped, raw[:, :, part * PIECE : (part + 1) * PIECE], vector_cols)
-            return grouped, mx_operand(keep, PIECE, label)
-
-        def quantise_piece(piece):
-            grouped, operand = piece
-            quantise(nc, operand, grouped[:].rearrange("p w t -> p (w t)"))
-
-        w_cq_mx = []
-        waiting = None
-        for c in range(PASSES_1):
-            w_cq_mx.append([])
-            for g in range(PASSES_2):
-                piece = regroup_piece(raw_tiles[c], g, VECTOR_COLS_BEFORE_ROPE, "w_cq%d%d" % (c, g), regroup_permuted)
-                w_cq_mx[c].append(piece[1])
-                if waiting is not None:
-                    quantise_piece(waiting)
-                waiting = piece
-            load_next_weights()
-        quantise_piece(waiting)
-        waiting = None
+        result_pool = ctx.enter_context(tc.tile_pool(name="result_pool", bufs=6, reuse_waits="tile"))
 
         c_q_grouped = {}
         c_q_mx = {}
-        w_mx = {}
-        products = {}
         results = {}
         out_rows = out.rearrange("b n (p a) d -> p (b n) a d", a=S_TILES)
 
         def step_of(j):
-            half, rest = divmod(j, S_TILES * PARTS)
-            a, part = divmod(rest, PARTS)
+            group, a = divmod(j, S_TILES)
+            half, part = divmod(group, PARTS)
             return half, part, a
 
         def c_q_bank(b):
-            a, g = divmod(b, PASSES_2)
-            bank = psum_c_q.tile([P, PACK, P], F32)
+            g, a = divmod(b, S_TILES)
+            bank = psum_main.tile([P, PACK, P], F32, tag="bank", name="c_q")
             for t in range(PACK):
                 for c in range(PASSES_1):
                     multiply_mx(
                         nc,
                         bank[:, t, :],
-                        columns(w_cq_mx[c][g], t * P, P),
+                        columns(w_cq_mx[(g, c)], t * P, P),
                         columns(h_mx[a], c * P, P),
                         first=(c == 0),
                         last=(c == PASSES_1 - 1),
@@ -263,7 +327,7 @@ def tile_mla_pa_kernel(tc, h, w_cq, w_q, w_qr, out):
             return bank
 
         def copy_c_q_bank(b, bank):
-            a, g = divmod(b, PASSES_2)
+            g, a = divmod(b, S_TILES)
             if g == 0:
                 c_q_grouped[a] = c_q_stage.tile([P, PASSES_2, P, PACK], BF16, align_bytes=64, name="c_q_grouped")
             nc.scalar.copy(out=c_q_grouped[a][:, g], in_=bank[:].rearrange("m t s -> m s t"))
@@ -272,9 +336,12 @@ def tile_mla_pa_kernel(tc, h, w_cq, w_q, w_qr, out):
             c_q_mx[a] = mx_operand(keep, PASSES_2 * P, "c_q%d" % a)
             quantise(nc, c_q_mx[a], c_q_grouped[a][:].rearrange("m g s t -> m (g s t)"))
 
-        def multiply_by_weights(j, weight, pool):
+        def multiply_by_weights(j, weight):
             half, part, a = step_of(j)
-            bank = pool.tile([P, GROUP_HEADS, D_HEAD], F32, name="bank%d" % weight, tag="u_bank" if weight == 0 else "a_bank")
+            if weight == 0:
+                bank = psum_main.tile([P, GROUP_HEADS, D_HEAD], F32, tag="bank", name="u")
+            else:
+                bank = psum_a.tile([P, GROUP_HEADS, D_HEAD], F32, name="a")
             for g in range(PASSES_2):
                 multiply_mx(
                     nc,
@@ -290,67 +357,51 @@ def tile_mla_pa_kernel(tc, h, w_cq, w_q, w_qr, out):
             a = step_of(j)[2]
             whole = [P, GROUP_HEADS, PAIRS, 2]
             u_pairs = u_bank[:].rearrange("p n (i e) -> p n i e", e=2)
-            from_even = rope_pool.tile(whole, F32)
-            nc.vector.tensor_tensor(
-                out=from_even[:],
-                in0=u_pairs[:, :, :, 0:1].to_broadcast(whole),
-                in1=for_even[:, a].unsqueeze(1).to_broadcast(whole),
-                op=ALU.mult,
-            )
-            from_odd = rope_pool.tile(whole, F32)
-            nc.vector.tensor_tensor(
-                out=from_odd[:],
-                in0=u_pairs[:, :, :, 1:2].to_broadcast(whole),
-                in1=for_odd[:, a].unsqueeze(1).to_broadcast(whole),
-                op=ALU.mult,
-            )
-            products[j] = (from_even, from_odd)
+            both = []
+            for e, pair in ((0, for_even), (1, for_odd)):
+                product = rope_pool.tile(whole, F32, name="product%d" % e)
+                nc.vector.tensor_tensor(
+                    out=product[:],
+                    in0=u_pairs[:, :, :, e : e + 1].to_broadcast(whole),
+                    in1=pair[:, :, a].rearrange("p e i -> p i e").unsqueeze(1).to_broadcast(whole),
+                    op=ALU.mult,
+                )
+                both.append(product[:].rearrange("p n i e -> p n (i e)"))
+            return both
 
-        def rope_sum(j):
-            from_even, from_odd = products[j]
+        def rope_sum(j, both):
             results[j] = result_pool.tile([P, GROUP_HEADS, 2 * D_HEAD], F32, name="result")
-            nc.gpsimd.tensor_tensor(
-                out=results[j][:, :, D_HEAD:],
-                in0=from_even[:].rearrange("p n i e -> p n (i e)"),
-                in1=from_odd[:].rearrange("p n i e -> p n (i e)"),
-                op=ALU.add,
-            )
+            nc.gpsimd.tensor_tensor(out=results[j][:, :, D_HEAD:], in0=both[0], in1=both[1], op=ALU.add)
 
         def store(j):
             half, part, a = step_of(j)
             first_head = (half * PARTS + part) * GROUP_HEADS
             nc.sync.dma_start(out=out_rows[:, first_head : first_head + GROUP_HEADS, a, :], in_=results[j][:])
 
-        for i in range(STEPS + A_LAG):
-            u_step, a_step = i - U_LAG, i - A_LAG
-            if i < C_Q_BANKS:
-                new_c_q = c_q_bank(i)
+        c_q_banks = {}
+        pass_through(2)
+        for n in range(2, A_START + STEPS):
+            b, u_step, a_step = n - C_Q_START, n - U_START, n - A_START
+            if 0 <= b < C_Q_BANKS:
+                c_q_banks[b] = c_q_bank(b)
             if 0 <= u_step < STEPS:
-                u_bank = multiply_by_weights(u_step, 0, psum_u)
-            if 0 <= a_step:
-                a_bank = multiply_by_weights(a_step, 1, psum_a)
-            piece = None
-            if i < PIECES:
-                load, part = divmod(i, PARTS)
-                half, rest = divmod(load, 2 * PASSES_2)
-                weight, g = divmod(rest, PASSES_2)
-                piece = regroup_piece(
-                    raw_tiles[PASSES_1 + load],
-                    part,
-                    VECTOR_COLS_BEFORE_ROPE if i < U_LAG else VECTOR_COLS_BESIDE_ROPE,
-                    "w%d%d%d%d" % (weight, half, part, g),
-                )
-                w_mx[(weight, half, part, g)] = piece[1]
-            if waiting is not None:
-                quantise_piece(waiting)
-            waiting = piece
-            if i < C_Q_BANKS:
-                copy_c_q_bank(i, new_c_q)
-            if 0 < i <= C_Q_BANKS and i % PASSES_2 == 0:
-                quantise_c_q(i // PASSES_2 - 1)
+                u_bank = multiply_by_weights(u_step, 0)
+            if 0 <= a_step < STEPS:
+                a_bank = multiply_by_weights(a_step, 1)
+            if n + 1 < CQ_PIECES + W_PIECES:
+                pass_through(n + 1)
+            if n < CQ_PIECES + W_PIECES:
+                regroup(n)
+                if n >= CQ_PIECES and (n - CQ_PIECES) % PARTS == PARTS - 1 and len(w_raw) < len(w_sources):
+                    load_w()
+            if 2 < n <= CQ_PIECES + W_PIECES:
+                quantise_piece(n - 1)
+            if 1 <= b <= C_Q_BANKS:
+                copy_c_q_bank(b - 1, c_q_banks[b - 1])
+            if C_Q_BANKS - S_TILES < b - 1 <= C_Q_BANKS:
+                quantise_c_q(b - 2 - (C_Q_BANKS - S_TILES))
             if 0 <= u_step < STEPS:
-                rope_products(u_step, u_bank)
-                rope_sum(u_step)
-            if 0 <= a_step:
+                rope_sum(u_step, rope_products(u_step, u_bank))
+            if 0 <= a_step < STEPS:
                 nc.scalar.copy(out=results[a_step][:, :, 0:D_HEAD], in_=a_bank[:])
                 store(a_step)

@@ -44,17 +44,14 @@ A_START = U_START + 4
 
 PSUM_MAIN = 6
 RAW_BUFS = 6
-UNIT = 4
-UNITS = PIECE // UNIT
-BANK_UNITS = 64
+RUN_COLS = P
+BANK_COLS = 2 * RUN_COLS
 
 
 def shares(n):
-    if n < PASSES_1:
-        return 32, 32
-    if n < CQ_PIECES + 3:
-        return 80, UNITS
-    return 20, BANK_UNITS
+    if n < CQ_PIECES:
+        return 2 * P, PIECE
+    return 176, PIECE
 
 
 ROUND_MAGIC = 1.5 * 2.0**23
@@ -190,58 +187,50 @@ def tile_mla_pa_kernel(tc, h, w_cq, w_q, w_qr, out):
         grouped_tiles = {}
         passed = {}
 
-        def views(n):
-            grouped = grouped_tiles[n]
+        def raw_columns(n, first, last):
             if n < CQ_PIECES:
-                src = cq_raw[n][:].rearrange("p j (m t) -> p m j t", t=UNIT)
-                return src, grouped[:].rearrange("p (t m) j -> p m j t", t=UNIT)
+                by_group = cq_raw[n][:].rearrange("p j (m t) -> p j t m", t=PACK)
+                return by_group[:, :, first // P : last // P]
             load, part = divmod(n - CQ_PIECES, PARTS)
-            src = w_raw[load][:, :, part * PIECE : (part + 1) * PIECE].rearrange("p j (m t) -> p m j t", t=UNIT)
-            return src, grouped[:].rearrange("p (m t) j -> p m j t", t=UNIT)
+            return w_raw[load][:, :, part * PIECE + first : part * PIECE + last]
 
         def pass_through(n):
-            grouped_tiles[n] = stage.tile([P, PIECE, PACK], BF16, align_bytes=64, name="grouped")
-            src, dst = views(n)
             passed[n] = []
-            first = shares(n)[1]
-            while first < UNITS:
-                width = min(BANK_UNITS, UNITS - first)
-                bank = psum_main.tile([P, width * UNIT * PACK], BF16, tag="bank", name="passed")
-                here = src[:, first : first + width]
-                if n < CQ_PIECES:
-                    here = here.rearrange("p m j t -> p t m j")
-                    to = grouped_tiles[n][:].rearrange("p (t m) j -> p t (m j)", t=UNIT)
-                    to = to[:, :, first * PACK : (first + width) * PACK]
-                    runs = UNIT * width * UNIT * PACK // (UNIT * 512)
-                    per = UNIT // runs
-                    moving = [here[:, r * per : (r + 1) * per] for r in range(runs)]
-                else:
-                    to = grouped_tiles[n][:].rearrange("p c j -> p (c j)")
-                    to = to[:, first * UNIT * PACK : (first + width) * UNIT * PACK]
-                    runs = width * UNIT * PACK // 512
-                    load, part = divmod(n - CQ_PIECES, PARTS)
-                    start = part * PIECE + first * UNIT
-                    cols = w_raw[load][:, :, start : start + width * UNIT].rearrange("p j c -> p c j")
-                    per = width * UNIT // runs
-                    moving = [cols[:, r * per : (r + 1) * per] for r in range(runs)]
-                for r in range(runs):
+            for first in range(shares(n)[1], PIECE, BANK_COLS):
+                last = min(first + BANK_COLS, PIECE)
+                bank = psum_main.tile([P, last - first, PACK], BF16, tag="bank", name="passed")
+                for start in range(first, last, RUN_COLS):
+                    rows = raw_columns(n, start, start + RUN_COLS)
+                    if n < CQ_PIECES:
+                        rows = rows[:, :, 0]
                     nc.tensor.matmul(
-                        bank[:, r * 512 : (r + 1) * 512], lhsT=identity_bf16[:], rhs=moving[r], start=True, stop=True
+                        bank[:, start - first : start - first + RUN_COLS].rearrange("p c j -> p (c j)"),
+                        lhsT=identity_bf16[:],
+                        rhs=rows.rearrange("p j c -> p c j"),
+                        start=True,
+                        stop=True,
                     )
-                words = bank[:].bitcast(F32)
-                if n < CQ_PIECES:
-                    words = words.rearrange("p (t w) -> p t w", t=UNIT)
-                passed[n].append((words, to.bitcast(F32)))
-                first += width
+                passed[n].append((first, last, bank))
 
         def regroup(n):
-            src, dst = views(n)
-            for words, to in passed[n]:
-                nc.scalar.copy(out=to, in_=words)
-            v, sc = shares(n)
-            nc.vector.tensor_copy(out=dst[:, :v], in_=src[:, :v])
-            if sc > v:
-                nc.scalar.copy(out=dst[:, v:sc], in_=src[:, v:sc])
+            grouped = stage.tile([P, PIECE, PACK], BF16, align_bytes=64, name="grouped")
+            grouped_tiles[n] = grouped
+            for first, last, bank in passed[n]:
+                nc.scalar.copy(
+                    out=grouped[:, first:last].rearrange("p c j -> p (c j)").bitcast(F32),
+                    in_=bank[:].rearrange("p c j -> p (c j)").bitcast(F32),
+                )
+            by_vector, by_scalar = shares(n)
+            for copy, first, last in ((nc.vector.tensor_copy, 0, by_vector), (nc.scalar.copy, by_vector, by_scalar)):
+                if first < last:
+                    dst, src = grouped[:, first:last], raw_columns(n, first, last)
+                    if n < CQ_PIECES:
+                        dst = dst.rearrange("p (t m) j -> p m j t", m=P)
+                        src = src.rearrange("p j t m -> p m j t")
+                    else:
+                        dst = dst.rearrange("p (w i) j -> p w j i", i=4)
+                        src = src.rearrange("p j (w i) -> p w j i", i=4)
+                    copy(out=dst, in_=src)
             if n < CQ_PIECES:
                 operand = mx_operand(keep, PIECE, "w_cq%d" % n)
                 w_cq_mx[divmod(n, PASSES_1)] = operand

@@ -43,7 +43,7 @@ U_START = CQ_PIECES + 4
 A_START = U_START + 4
 
 PSUM_MAIN = 6
-RAW_BUFS = 6
+RAW_BUFS = 5
 RUN_COLS = P
 BANK_COLS = 2 * RUN_COLS
 
@@ -55,6 +55,8 @@ def shares(n):
 
 
 ROUND_MAGIC = 1.5 * 2.0**23
+
+STORE_TILES = 2
 
 FLOPS = 2 * S * D_MODEL * D_CQ + 2 * S * D_CQ * 2 * HEADS * D_HEAD
 
@@ -288,7 +290,7 @@ def tile_mla_pa_kernel(tc, h, w_cq, w_q, w_qr, out):
                     quantise(nc, h_mx[a - 1], h_grouped[a - 1][:].rearrange("q c s t -> q (c s t)"))
             quantise(nc, h_mx[-1], h_grouped[-1][:].rearrange("q c s t -> q (c s t)"))
         rope_pool = ctx.enter_context(tc.tile_pool(name="rope_pool", bufs=4, reuse_waits="tile"))
-        result_pool = ctx.enter_context(tc.tile_pool(name="result_pool", bufs=6, reuse_waits="tile"))
+        result_pool = ctx.enter_context(tc.tile_pool(name="result_pool", bufs=4, reuse_waits="tile"))
 
         c_q_grouped = {}
         c_q_mx = {}
@@ -358,14 +360,21 @@ def tile_mla_pa_kernel(tc, h, w_cq, w_q, w_qr, out):
                 both.append(product[:].rearrange("p n i e -> p n (i e)"))
             return both
 
+        def result_of(j):
+            return results[j // STORE_TILES][:, :, j % STORE_TILES]
+
         def rope_sum(j, both):
-            results[j] = result_pool.tile([P, GROUP_HEADS, 2 * D_HEAD], F32, name="result")
-            nc.gpsimd.tensor_tensor(out=results[j][:, :, D_HEAD:], in0=both[0], in1=both[1], op=ALU.add)
+            if j % STORE_TILES == 0:
+                results[j // STORE_TILES] = result_pool.tile([P, GROUP_HEADS, STORE_TILES, 2 * D_HEAD], F32, name="result")
+            nc.gpsimd.tensor_tensor(out=result_of(j)[:, :, D_HEAD:], in0=both[0], in1=both[1], op=ALU.add)
 
         def store(j):
             half, part, a = step_of(j)
             first_head = (half * PARTS + part) * GROUP_HEADS
-            nc.sync.dma_start(out=out_rows[:, first_head : first_head + GROUP_HEADS, a, :], in_=results[j][:])
+            tiles = slice(a + 1 - STORE_TILES, a + 1)
+            nc.sync.dma_start(
+                out=out_rows[:, first_head : first_head + GROUP_HEADS, tiles, :], in_=results[j // STORE_TILES][:]
+            )
 
         c_q_banks = {}
         pass_through(2)
@@ -392,5 +401,6 @@ def tile_mla_pa_kernel(tc, h, w_cq, w_q, w_qr, out):
             if 0 <= u_step < STEPS:
                 rope_sum(u_step, rope_products(u_step, u_bank))
             if 0 <= a_step < STEPS:
-                nc.scalar.copy(out=results[a_step][:, :, 0:D_HEAD], in_=a_bank[:])
-                store(a_step)
+                nc.scalar.copy(out=result_of(a_step)[:, :, 0:D_HEAD], in_=a_bank[:])
+                if a_step % STORE_TILES == STORE_TILES - 1:
+                    store(a_step)

@@ -34,12 +34,15 @@ GROUP_HEADS = PIECE // D_HEAD
 HALVES = HEADS * D_HEAD // LOAD_COLS
 
 CQ_PIECES = PASSES_2 * PASSES_1
+CQ_ORDER = [(g, c) for c in range(PASSES_1 // 2) for g in range(PASSES_2)] + [
+    (g, c) for g in range(PASSES_2) for c in range(PASSES_1 // 2, PASSES_1)
+]
 C_Q_BANKS = PASSES_2 * S_TILES
 W_PIECES = 2 * PASSES_2 * HALVES * PARTS
 STEPS = S_TILES * HALVES * PARTS
 
-C_Q_START = PASSES_1 + 1
-U_START = CQ_PIECES + 4
+C_Q_START = CQ_ORDER.index((0, PASSES_1 - 1)) + 1
+U_START = C_Q_START + C_Q_BANKS - 1
 A_START = U_START + 4
 
 PSUM_MAIN = 6
@@ -51,7 +54,9 @@ BANK_COLS = 2 * RUN_COLS
 def shares(n):
     if n < CQ_PIECES:
         return 2 * P, PIECE
-    return 176, PIECE
+    if n < U_START:
+        return 256, PIECE
+    return 144, PIECE
 
 
 ROUND_MAGIC = 1.5 * 2.0**23
@@ -93,7 +98,7 @@ def tile_mla_pa_kernel(tc, h, w_cq, w_q, w_qr, out):
         ctx.enter_context(tc.manual_schedule())
         const = ctx.enter_context(tc.tile_pool(name="const", bufs=1))
         keep = ctx.enter_context(tc.tile_pool(name="keep", bufs=1))
-        cq_raw_pool = ctx.enter_context(tc.tile_pool(name="cq_raw_pool", bufs=CQ_PIECES))
+        cq_raw_pool = ctx.enter_context(tc.tile_pool(name="cq_raw_pool", bufs=PASSES_1))
         raw_pool = ctx.enter_context(tc.tile_pool(name="raw_pool", bufs=RAW_BUFS))
         stage = ctx.enter_context(tc.tile_pool(name="stage", bufs=4))
         c_q_stage = ctx.enter_context(tc.tile_pool(name="c_q_stage", bufs=S_TILES))
@@ -104,10 +109,14 @@ def tile_mla_pa_kernel(tc, h, w_cq, w_q, w_qr, out):
         cq_raw = []
 
         def load_w_cq():
-            g, c = divmod(len(cq_raw), PASSES_1)
-            raw = cq_raw_pool.tile([P, PACK, PIECE], BF16, name="cq_raw")
-            nc.sync.dma_start(out=raw[:], in_=w_cq_rows[c][:, :, g * PIECE : (g + 1) * PIECE])
+            c = len(cq_raw)
+            raw = cq_raw_pool.tile([P, PACK, D_CQ], BF16, name="cq_raw")
             cq_raw.append(raw)
+            loads = PASSES_2 if c == 0 else 1
+            width = D_CQ // loads
+            for part in range(loads):
+                cols = slice(part * width, (part + 1) * width)
+                nc.sync.dma_start(out=raw[:, :, cols], in_=w_cq_rows[c][:, :, cols])
 
         h_rows = h.flatten_outer_dims().rearrange("(p a) k -> p a k", a=S_TILES)
         h_mx = []
@@ -175,12 +184,16 @@ def tile_mla_pa_kernel(tc, h, w_cq, w_q, w_qr, out):
         nc.vector.tensor_tensor(out=turns[:], in0=turns[:], in1=whole_turns[:], op=ALU.subtract)
         nc.scalar.activation(out=sin_half[:], in_=turns[:], func=ACT.Sin, scale=math.pi)
         nc.scalar.activation(out=sin_quarter[:], in_=turns[:], func=ACT.Sin, scale=math.pi / 2.0)
-        for sine, cosine in ((sin_half[:], factors[:, 1]), (sin_quarter[:], cos_half[:])):
-            nc.gpsimd.tensor_tensor(out=square[:], in0=sine, in1=sine, op=ALU.mult)
-            nc.gpsimd.tensor_scalar(out=cosine, in0=square[:], scalar1=-2.0, scalar2=1.0, op0=ALU.mult, op1=ALU.add)
-        nc.gpsimd.tensor_tensor(out=square[:], in0=sin_half[:], in1=cos_half[:], op=ALU.mult)
-        for sign, plane in ((2.0, 2), (-2.0, 0)):
-            nc.gpsimd.tensor_scalar(out=factors[:, plane], in0=square[:], scalar1=sign, scalar2=0.0, op0=ALU.mult, op1=ALU.add)
+        nc.scalar.activation(out=square[:], in_=sin_half[:], func=ACT.Square)
+        nc.scalar.activation(out=cos_half[:], in_=sin_quarter[:], func=ACT.Square)
+
+        def rope_factors():
+            for squared, cosine in ((square[:], factors[:, 1]), (cos_half[:], cos_half[:])):
+                nc.vector.tensor_scalar(out=cosine, in0=squared, scalar1=-2.0, scalar2=1.0, op0=ALU.mult, op1=ALU.add)
+            for factor, plane in ((2.0, 2), (-2.0, 0)):
+                nc.vector.scalar_tensor_tensor(
+                    out=factors[:, plane], in0=sin_half[:], scalar=factor, in1=cos_half[:], op0=ALU.mult, op1=ALU.mult
+                )
 
         pieces = []
         w_cq_mx = {}
@@ -191,7 +204,9 @@ def tile_mla_pa_kernel(tc, h, w_cq, w_q, w_qr, out):
 
         def raw_columns(n, first, last):
             if n < CQ_PIECES:
-                by_group = cq_raw[n][:].rearrange("p j (m t) -> p j t m", t=PACK)
+                g, c = CQ_ORDER[n]
+                piece = cq_raw[c][:, :, g * PIECE : (g + 1) * PIECE]
+                by_group = piece.rearrange("p j (m t) -> p j t m", t=PACK)
                 return by_group[:, :, first // P : last // P]
             load, part = divmod(n - CQ_PIECES, PARTS)
             return w_raw[load][:, :, part * PIECE + first : part * PIECE + last]
@@ -235,7 +250,7 @@ def tile_mla_pa_kernel(tc, h, w_cq, w_q, w_qr, out):
                     copy(out=dst, in_=src)
             if n < CQ_PIECES:
                 operand = mx_operand(keep, PIECE, "w_cq%d" % n)
-                w_cq_mx[divmod(n, PASSES_1)] = operand
+                w_cq_mx[CQ_ORDER[n]] = operand
             else:
                 load, part = divmod(n - CQ_PIECES, PARTS)
                 half, rest = divmod(load, 2 * PASSES_2)
@@ -250,13 +265,12 @@ def tile_mla_pa_kernel(tc, h, w_cq, w_q, w_qr, out):
 
         with tc.tile_pool(name="h_pool", bufs=S_TILES) as h_pool, tc.tile_pool(name="h_stage", bufs=S_TILES) as h_stage:
             load_w_cq()
-            load_w_cq()
             h_raw = []
             for a in range(S_TILES):
                 h_tile = h_pool.tile([P, D_MODEL], BF16)
                 nc.sync.dma_start(out=h_tile[:], in_=h_rows[:, a, :])
                 h_raw.append(h_tile)
-            while len(cq_raw) < CQ_PIECES:
+            while len(cq_raw) < PASSES_1:
                 load_w_cq()
             for j in range(RAW_BUFS):
                 load_w()
@@ -286,6 +300,7 @@ def tile_mla_pa_kernel(tc, h, w_cq, w_q, w_qr, out):
                 h_mx.append(mx_operand(keep, PASSES_1 * P, "h%d" % a))
                 if a == 0:
                     quantise_piece(1)
+                    rope_factors()
                 else:
                     quantise(nc, h_mx[a - 1], h_grouped[a - 1][:].rearrange("q c s t -> q (c s t)"))
             quantise(nc, h_mx[-1], h_grouped[-1][:].rearrange("q c s t -> q (c s t)"))
@@ -380,8 +395,6 @@ def tile_mla_pa_kernel(tc, h, w_cq, w_q, w_qr, out):
         pass_through(2)
         for n in range(2, A_START + STEPS):
             b, u_step, a_step = n - C_Q_START, n - U_START, n - A_START
-            if 0 <= b < C_Q_BANKS:
-                c_q_banks[b] = c_q_bank(b)
             if 0 <= u_step < STEPS:
                 u_bank = multiply_by_weights(u_step, 0)
             if 0 <= a_step < STEPS:
@@ -394,6 +407,8 @@ def tile_mla_pa_kernel(tc, h, w_cq, w_q, w_qr, out):
                     load_w()
             if 2 < n <= CQ_PIECES + W_PIECES:
                 quantise_piece(n - 1)
+            if 0 <= b < C_Q_BANKS:
+                c_q_banks[b] = c_q_bank(b)
             if 1 <= b <= C_Q_BANKS:
                 copy_c_q_bank(b - 1, c_q_banks[b - 1])
             if C_Q_BANKS - S_TILES < b - 1 <= C_Q_BANKS:

@@ -37,26 +37,31 @@ CQ_PIECES = PASSES_2 * PASSES_1
 CQ_ORDER = [(g, c) for c in range(PASSES_1 // 2) for g in range(PASSES_2)] + [
     (g, c) for g in range(PASSES_2) for c in range(PASSES_1 // 2, PASSES_1)
 ]
+W_ORDER = [(weight, 0, part, g) for weight in range(2) for part in range(PARTS) for g in range(PASSES_2)] + [
+    (weight, 1, part, g) for part in range(PARTS) for weight in range(2) for g in range(PASSES_2)
+]
+C_Q_ORDER = [(g, a) for g in range(PASSES_2) for a in range(S_TILES // 2)] + [
+    (g, a) for a in range(S_TILES // 2, S_TILES) for g in range(PASSES_2)
+]
 C_Q_BANKS = PASSES_2 * S_TILES
 W_PIECES = 2 * PASSES_2 * HALVES * PARTS
 STEPS = S_TILES * HALVES * PARTS
 
 C_Q_START = CQ_ORDER.index((0, PASSES_1 - 1)) + 1
-U_START = C_Q_START + C_Q_BANKS - 1
-A_START = U_START + 4
+ROPE_START = C_Q_START + C_Q_ORDER.index((1, 0)) + 3
 
 PSUM_MAIN = 6
+V1, V2 = 256, 176
+A_PAIRS_START = CQ_PIECES + W_ORDER.index((1, 1, 0, 1)) + 2
 RAW_BUFS = 5
-RUN_COLS = P
-BANK_COLS = 2 * RUN_COLS
 
 
-def shares(n):
+def vector_columns(n):
+    if n < 2:
+        return 3 * P
     if n < CQ_PIECES:
-        return 2 * P, PIECE
-    if n < U_START:
-        return 256, PIECE
-    return 144, PIECE
+        return 2 * P
+    return V1 if n < ROPE_START else V2
 
 
 ROUND_MAGIC = 1.5 * 2.0**23
@@ -64,6 +69,24 @@ ROUND_MAGIC = 1.5 * 2.0**23
 STORE_TILES = 2
 
 FLOPS = 2 * S * D_MODEL * D_CQ + 2 * S * D_CQ * 2 * HEADS * D_HEAD
+
+
+def schedule(weight):
+    waiting = [(half, part, a) for half in range(HALVES) for part in range(PARTS) for a in range(S_TILES)]
+    iterations = {}
+    n = 0
+    while waiting:
+        iterations[n] = []
+        for step in list(waiting):
+            half, part, a = step
+            weights_ready = CQ_PIECES + W_ORDER.index((weight, half, part, PASSES_2 - 1)) + 2
+            c_q_ready = C_Q_START + C_Q_ORDER.index((PASSES_2 - 1, a)) + 3
+            room = 2 if weight == 1 and n >= A_PAIRS_START else 1
+            if n >= weights_ready and n >= c_q_ready and len(iterations[n]) < room:
+                iterations[n].append(step)
+                waiting.remove(step)
+        n += 1
+    return iterations
 
 
 def quantise(nc, operand, grouped):
@@ -112,26 +135,19 @@ def tile_mla_pa_kernel(tc, h, w_cq, w_q, w_qr, out):
             c = len(cq_raw)
             raw = cq_raw_pool.tile([P, PACK, D_CQ], BF16, name="cq_raw")
             cq_raw.append(raw)
-            loads = PASSES_2 if c == 0 else 1
-            width = D_CQ // loads
-            for part in range(loads):
-                cols = slice(part * width, (part + 1) * width)
-                nc.sync.dma_start(out=raw[:, :, cols], in_=w_cq_rows[c][:, :, cols])
+            nc.sync.dma_start(out=raw[:], in_=w_cq_rows[c])
 
         h_rows = h.flatten_outer_dims().rearrange("(p a) k -> p a k", a=S_TILES)
         h_mx = []
-        w_sources = []
-        for half in range(HALVES):
-            for weight in (w_qr, w_q):
-                rows = weight.rearrange("(g p t) n -> g p t n", g=PASSES_2, t=PACK)
-                for g in range(PASSES_2):
-                    w_sources.append(rows[g][:, :, half * LOAD_COLS : (half + 1) * LOAD_COLS])
-        w_raw = []
+        w_rows = [w.rearrange("(g p t) n -> g p t n", g=PASSES_2, t=PACK) for w in (w_qr, w_q)]
+        w_raw = {}
 
         def load_w():
+            half, rest = divmod(len(w_raw), 2 * PASSES_2)
+            weight, g = divmod(rest, PASSES_2)
             raw = raw_pool.tile([P, PACK, LOAD_COLS], BF16, name="w_raw")
-            nc.sync.dma_start(out=raw[:], in_=w_sources[len(w_raw)])
-            w_raw.append(raw)
+            nc.sync.dma_start(out=raw[:], in_=w_rows[weight][g][:, :, half * LOAD_COLS : (half + 1) * LOAD_COLS])
+            w_raw[(weight, half, g)] = raw
 
         zero = const.tile([P, 1], F32)
         nc.gpsimd.memset(zero[:], 0.0)
@@ -149,8 +165,6 @@ def tile_mla_pa_kernel(tc, h, w_cq, w_q, w_qr, out):
         )
         identity = const.tile([P, P], F32)
         make_identity(nc, identity[:])
-        identity_bf16 = const.tile([P, P], BF16)
-        nc.gpsimd.tensor_copy(out=identity_bf16[:], in_=identity[:])
         nc.vector.tensor_scalar_mul(out=position[:], in0=position[:], scalar1=1.0 / (2.0 * math.pi))
         frequency = const.tile([P, PAIRS], F32)
         nc.vector.memset(frequency[:, 0:1], 1.0)
@@ -182,10 +196,12 @@ def tile_mla_pa_kernel(tc, h, w_cq, w_q, w_qr, out):
             out=whole_turns[:], in0=turns[:], scalar1=ROUND_MAGIC, scalar2=ROUND_MAGIC, op0=ALU.add, op1=ALU.subtract
         )
         nc.vector.tensor_tensor(out=turns[:], in0=turns[:], in1=whole_turns[:], op=ALU.subtract)
-        nc.scalar.activation(out=sin_half[:], in_=turns[:], func=ACT.Sin, scale=math.pi)
-        nc.scalar.activation(out=sin_quarter[:], in_=turns[:], func=ACT.Sin, scale=math.pi / 2.0)
-        nc.scalar.activation(out=square[:], in_=sin_half[:], func=ACT.Square)
-        nc.scalar.activation(out=cos_half[:], in_=sin_quarter[:], func=ACT.Square)
+
+        def rope_sines():
+            nc.scalar.activation(out=sin_half[:], in_=turns[:], func=ACT.Sin, scale=math.pi)
+            nc.scalar.activation(out=sin_quarter[:], in_=turns[:], func=ACT.Sin, scale=math.pi / 2.0)
+            nc.scalar.activation(out=square[:], in_=sin_half[:], func=ACT.Square)
+            nc.scalar.activation(out=cos_half[:], in_=sin_quarter[:], func=ACT.Square)
 
         def rope_factors():
             for squared, cosine in ((square[:], factors[:, 1]), (cos_half[:], cos_half[:])):
@@ -199,8 +215,6 @@ def tile_mla_pa_kernel(tc, h, w_cq, w_q, w_qr, out):
         w_cq_mx = {}
         w_mx = {}
 
-        grouped_tiles = {}
-        passed = {}
 
         def raw_columns(n, first, last):
             if n < CQ_PIECES:
@@ -208,56 +222,30 @@ def tile_mla_pa_kernel(tc, h, w_cq, w_q, w_qr, out):
                 piece = cq_raw[c][:, :, g * PIECE : (g + 1) * PIECE]
                 by_group = piece.rearrange("p j (m t) -> p j t m", t=PACK)
                 return by_group[:, :, first // P : last // P]
-            load, part = divmod(n - CQ_PIECES, PARTS)
-            return w_raw[load][:, :, part * PIECE + first : part * PIECE + last]
-
-        def pass_through(n):
-            passed[n] = []
-            for first in range(shares(n)[1], PIECE, BANK_COLS):
-                last = min(first + BANK_COLS, PIECE)
-                bank = psum_main.tile([P, last - first, PACK], BF16, tag="bank", name="passed")
-                for start in range(first, last, RUN_COLS):
-                    rows = raw_columns(n, start, start + RUN_COLS)
-                    if n < CQ_PIECES:
-                        rows = rows[:, :, 0]
-                    nc.tensor.matmul(
-                        bank[:, start - first : start - first + RUN_COLS].rearrange("p c j -> p (c j)"),
-                        lhsT=identity_bf16[:],
-                        rhs=rows.rearrange("p j c -> p c j"),
-                        start=True,
-                        stop=True,
-                    )
-                passed[n].append((first, last, bank))
+            weight, half, part, g = W_ORDER[n - CQ_PIECES]
+            start = part * PIECE
+            return w_raw[(weight, half, g)][:, :, start + first : start + last]
 
         def regroup(n):
             grouped = stage.tile([P, PIECE, PACK], BF16, align_bytes=64, name="grouped")
-            grouped_tiles[n] = grouped
-            for first, last, bank in passed[n]:
-                nc.scalar.copy(
-                    out=grouped[:, first:last].rearrange("p c j -> p (c j)").bitcast(F32),
-                    in_=bank[:].rearrange("p c j -> p (c j)").bitcast(F32),
-                )
-            by_vector, by_scalar = shares(n)
-            for copy, first, last in ((nc.vector.tensor_copy, 0, by_vector), (nc.scalar.copy, by_vector, by_scalar)):
-                if first < last:
-                    dst, src = grouped[:, first:last], raw_columns(n, first, last)
-                    if n < CQ_PIECES:
-                        dst = dst.rearrange("p (t m) j -> p m j t", m=P)
-                        src = src.rearrange("p j t m -> p m j t")
-                    else:
-                        dst = dst.rearrange("p (w i) j -> p w j i", i=4)
-                        src = src.rearrange("p j (w i) -> p w j i", i=4)
-                    copy(out=dst, in_=src)
+            split = vector_columns(n)
+            for copy, first, last in ((nc.vector.tensor_copy, 0, split), (nc.scalar.copy, split, PIECE)):
+                dst, src = grouped[:, first:last], raw_columns(n, first, last)
+                if n < CQ_PIECES:
+                    dst = dst.rearrange("p (t m) j -> p m j t", m=P)
+                    src = src.rearrange("p j t m -> p m j t")
+                else:
+                    dst = dst.rearrange("p (w i) j -> p w j i", i=4)
+                    src = src.rearrange("p j (w i) -> p w j i", i=4)
+                copy(out=dst, in_=src)
             if n < CQ_PIECES:
                 operand = mx_operand(keep, PIECE, "w_cq%d" % n)
                 w_cq_mx[CQ_ORDER[n]] = operand
             else:
-                load, part = divmod(n - CQ_PIECES, PARTS)
-                half, rest = divmod(load, 2 * PASSES_2)
-                weight, g = divmod(rest, PASSES_2)
+                weight, half, part, g = W_ORDER[n - CQ_PIECES]
                 operand = mx_operand(keep, PIECE, "w%d%d%d%d" % (weight, half, part, g))
                 w_mx[(weight, half, part, g)] = operand
-            pieces.append((grouped_tiles[n], operand))
+            pieces.append((grouped, operand))
 
         def quantise_piece(n):
             grouped, operand = pieces[n]
@@ -275,10 +263,9 @@ def tile_mla_pa_kernel(tc, h, w_cq, w_q, w_qr, out):
             for j in range(RAW_BUFS):
                 load_w()
 
-            pass_through(0)
-            pass_through(1)
             regroup(0)
             regroup(1)
+            rope_sines()
             quantise_piece(0)
             h_grouped = []
             for a in range(S_TILES):
@@ -293,10 +280,7 @@ def tile_mla_pa_kernel(tc, h, w_cq, w_q, w_qr, out):
                         nc.tensor.transpose(flipped[:, j, :], words, identity[:])
                     target = grouped_a[:, 2 * b : 2 * b + 2].bitcast(F32)
                     flipped_words = flipped[:].rearrange("q (c u) s -> q c s u", u=2)
-                    if b == 0:
-                        nc.scalar.copy(out=target, in_=flipped_words)
-                    else:
-                        nc.vector.tensor_copy(out=target, in_=flipped_words)
+                    nc.scalar.copy(out=target, in_=flipped_words)
                 h_mx.append(mx_operand(keep, PASSES_1 * P, "h%d" % a))
                 if a == 0:
                     quantise_piece(1)
@@ -304,21 +288,16 @@ def tile_mla_pa_kernel(tc, h, w_cq, w_q, w_qr, out):
                 else:
                     quantise(nc, h_mx[a - 1], h_grouped[a - 1][:].rearrange("q c s t -> q (c s t)"))
             quantise(nc, h_mx[-1], h_grouped[-1][:].rearrange("q c s t -> q (c s t)"))
-        rope_pool = ctx.enter_context(tc.tile_pool(name="rope_pool", bufs=4, reuse_waits="tile"))
-        result_pool = ctx.enter_context(tc.tile_pool(name="result_pool", bufs=4, reuse_waits="tile"))
+        rope_pool = ctx.enter_context(tc.tile_pool(name="rope_pool", bufs=3, reuse_waits="tile"))
+        result_pool = ctx.enter_context(tc.tile_pool(name="result_pool", bufs=5, reuse_waits="tile"))
 
         c_q_grouped = {}
         c_q_mx = {}
         results = {}
         out_rows = out.rearrange("b n (p a) d -> p (b n) a d", a=S_TILES)
 
-        def step_of(j):
-            group, a = divmod(j, S_TILES)
-            half, part = divmod(group, PARTS)
-            return half, part, a
-
         def c_q_bank(b):
-            g, a = divmod(b, S_TILES)
+            g, a = C_Q_ORDER[b]
             bank = psum_main.tile([P, PACK, P], F32, tag="bank", name="c_q")
             for t in range(PACK):
                 for c in range(PASSES_1):
@@ -333,7 +312,7 @@ def tile_mla_pa_kernel(tc, h, w_cq, w_q, w_qr, out):
             return bank
 
         def copy_c_q_bank(b, bank):
-            g, a = divmod(b, S_TILES)
+            g, a = C_Q_ORDER[b]
             if g == 0:
                 c_q_grouped[a] = c_q_stage.tile([P, PASSES_2, P, PACK], BF16, align_bytes=64, name="c_q_grouped")
             nc.scalar.copy(out=c_q_grouped[a][:, g], in_=bank[:].rearrange("m t s -> m s t"))
@@ -342,8 +321,8 @@ def tile_mla_pa_kernel(tc, h, w_cq, w_q, w_qr, out):
             c_q_mx[a] = mx_operand(keep, PASSES_2 * P, "c_q%d" % a)
             quantise(nc, c_q_mx[a], c_q_grouped[a][:].rearrange("m g s t -> m (g s t)"))
 
-        def multiply_by_weights(j, weight):
-            half, part, a = step_of(j)
+        def multiply_by_weights(step, weight):
+            half, part, a = step
             if weight == 0:
                 bank = psum_main.tile([P, GROUP_HEADS, D_HEAD], F32, tag="bank", name="u")
             else:
@@ -359,8 +338,7 @@ def tile_mla_pa_kernel(tc, h, w_cq, w_q, w_qr, out):
                 )
             return bank
 
-        def rope_products(j, u_bank):
-            a = step_of(j)[2]
+        def rope_products(a, u_bank):
             whole = [P, GROUP_HEADS, PAIRS, 2]
             u_pairs = u_bank[:].rearrange("p n (i e) -> p n i e", e=2)
             both = []
@@ -375,35 +353,36 @@ def tile_mla_pa_kernel(tc, h, w_cq, w_q, w_qr, out):
                 both.append(product[:].rearrange("p n i e -> p n (i e)"))
             return both
 
-        def result_of(j):
-            return results[j // STORE_TILES][:, :, j % STORE_TILES]
+        def result_of(step):
+            half, part, a = step
+            key = (half, part, a // STORE_TILES)
+            if key not in results:
+                results[key] = result_pool.tile([P, GROUP_HEADS, STORE_TILES, 2 * D_HEAD], F32, name="result")
+            return results[key][:, :, a % STORE_TILES]
 
-        def rope_sum(j, both):
-            if j % STORE_TILES == 0:
-                results[j // STORE_TILES] = result_pool.tile([P, GROUP_HEADS, STORE_TILES, 2 * D_HEAD], F32, name="result")
-            nc.gpsimd.tensor_tensor(out=result_of(j)[:, :, D_HEAD:], in0=both[0], in1=both[1], op=ALU.add)
+        def rope_sum(engine, step, both):
+            engine.tensor_tensor(out=result_of(step)[:, :, D_HEAD:], in0=both[0], in1=both[1], op=ALU.add)
 
-        def store(j):
-            half, part, a = step_of(j)
+        def store(step, tiles):
+            half, part, a = step
             first_head = (half * PARTS + part) * GROUP_HEADS
-            tiles = slice(a + 1 - STORE_TILES, a + 1)
+            last = a % STORE_TILES + 1
             nc.sync.dma_start(
-                out=out_rows[:, first_head : first_head + GROUP_HEADS, tiles, :], in_=results[j // STORE_TILES][:]
+                out=out_rows[:, first_head : first_head + GROUP_HEADS, a + 1 - tiles : a + 1, :],
+                in_=results[(half, part, a // STORE_TILES)][:, :, last - tiles : last],
             )
 
         c_q_banks = {}
-        pass_through(2)
-        for n in range(2, A_START + STEPS):
-            b, u_step, a_step = n - C_Q_START, n - U_START, n - A_START
-            if 0 <= u_step < STEPS:
-                u_bank = multiply_by_weights(u_step, 0)
-            if 0 <= a_step < STEPS:
-                a_bank = multiply_by_weights(a_step, 1)
-            if n + 1 < CQ_PIECES + W_PIECES:
-                pass_through(n + 1)
+        u_schedule, a_schedule = schedule(0), schedule(1)
+        last_iteration = max(a_schedule)
+        for n in range(2, last_iteration + 1):
+            b = n - C_Q_START
+            u_steps, a_steps = u_schedule.get(n, []), a_schedule.get(n, [])
+            u_banks = [multiply_by_weights(step, 0) for step in u_steps]
+            a_banks = [multiply_by_weights(step, 1) for step in a_steps]
             if n < CQ_PIECES + W_PIECES:
                 regroup(n)
-                if n >= CQ_PIECES and (n - CQ_PIECES) % PARTS == PARTS - 1 and len(w_raw) < len(w_sources):
+                if n >= CQ_PIECES and W_ORDER[n - CQ_PIECES][2] == PARTS - 1 and len(w_raw) < W_PIECES // PARTS:
                     load_w()
             if 2 < n <= CQ_PIECES + W_PIECES:
                 quantise_piece(n - 1)
@@ -411,11 +390,14 @@ def tile_mla_pa_kernel(tc, h, w_cq, w_q, w_qr, out):
                 c_q_banks[b] = c_q_bank(b)
             if 1 <= b <= C_Q_BANKS:
                 copy_c_q_bank(b - 1, c_q_banks[b - 1])
-            if C_Q_BANKS - S_TILES < b - 1 <= C_Q_BANKS:
-                quantise_c_q(b - 2 - (C_Q_BANKS - S_TILES))
-            if 0 <= u_step < STEPS:
-                rope_sum(u_step, rope_products(u_step, u_bank))
-            if 0 <= a_step < STEPS:
-                nc.scalar.copy(out=result_of(a_step)[:, :, 0:D_HEAD], in_=a_bank[:])
-                if a_step % STORE_TILES == STORE_TILES - 1:
-                    store(a_step)
+            if 2 <= b <= C_Q_BANKS + 1 and C_Q_ORDER[b - 2][0] == PASSES_2 - 1:
+                quantise_c_q(C_Q_ORDER[b - 2][1])
+            for step, bank in zip(u_steps, u_banks):
+                engine = nc.vector if n == last_iteration else nc.gpsimd
+                rope_sum(engine, step, rope_products(step[2], bank))
+            for step, bank in zip(a_steps, a_banks):
+                nc.scalar.copy(out=result_of(step)[:, :, 0:D_HEAD], in_=bank[:])
+                if n == last_iteration:
+                    store(step, 1)
+                elif step[2] % STORE_TILES == STORE_TILES - 1:
+                    store(step, STORE_TILES)

@@ -28,61 +28,54 @@ S_TILES = S // P
 PASSES_1 = D_MODEL // K_PASS
 PASSES_2 = D_CQ // K_PASS
 PIECE = 512
-LOAD_COLS = 2 * PIECE
-PARTS = LOAD_COLS // PIECE
+PARTS = 2
+LOAD_COLS = PARTS * PIECE
 GROUP_HEADS = PIECE // D_HEAD
-HALVES = HEADS * D_HEAD // LOAD_COLS
+GROUPS = HEADS // GROUP_HEADS
 
-CQ_PIECES = PASSES_2 * PASSES_1
-CQ_ORDER = [(g, c) for c in range(PASSES_1 // 2) for g in range(PASSES_2)] + [
-    (g, c) for g in range(PASSES_2) for c in range(PASSES_1 // 2, PASSES_1)
+LOADS = [("w_cq", 0, k) for k in range(PASSES_1)] + [
+    (weight, half, g) for half in range(2) for weight in ("w_qr", "w_q") for g in range(PASSES_2)
 ]
-W_ORDER = [(weight, 0, part, g) for weight in range(2) for part in range(PARTS) for g in range(PASSES_2)] + [
-    (weight, 1, part, g) for part in range(PARTS) for weight in range(2) for g in range(PASSES_2)
-]
-C_Q_ORDER = [(g, a) for g in range(PASSES_2) for a in range(S_TILES // 2)] + [
-    (g, a) for a in range(S_TILES // 2, S_TILES) for g in range(PASSES_2)
-]
-C_Q_BANKS = PASSES_2 * S_TILES
-W_PIECES = 2 * PASSES_2 * HALVES * PARTS
-STEPS = S_TILES * HALVES * PARTS
+H_LOAD = PASSES_1 - 1
+PIECES = [("w_cq", q, k) for k in range(PASSES_1) for q in range(PASSES_2)] + [
+    (weight, q, g) for weight in ("w_qr", "w_q") for q in (0, 1) for g in range(PASSES_2)
+] + [(weight, q, g) for q in (2, 3) for weight in ("w_qr", "w_q") for g in range(PASSES_2)]
+BEFORE_H = H_LOAD * PARTS
+C_Q_BANKS = [(g, a) for a in range(S_TILES) for g in range(PASSES_2)]
 
-C_Q_START = CQ_ORDER.index((0, PASSES_1 - 1)) + 1
-ROPE_START = C_Q_START + C_Q_ORDER.index((1, 0)) + 3
-
+C_Q_START = PIECES.index(("w_cq", 0, PASSES_1 - 1)) + 1
+C_Q_ITERATION = {bank: C_Q_START + i - (i >= 2) for i, bank in enumerate(C_Q_BANKS)}
+A_PAIRS_START = PIECES.index(("w_q", 2, 1)) + 2
+V1, V2 = 256, 144
+RAW_BUFS = 9
+STORE_TILES = 2
 PSUM_MAIN = 6
-V1, V2 = 256, 176
-A_PAIRS_START = CQ_PIECES + W_ORDER.index((1, 1, 0, 1)) + 2
-RAW_BUFS = 5
-
-
-def vector_columns(n):
-    if n < 2:
-        return 3 * P
-    if n < CQ_PIECES:
-        return 2 * P
-    return V1 if n < ROPE_START else V2
-
 
 ROUND_MAGIC = 1.5 * 2.0**23
-
-STORE_TILES = 2
 
 FLOPS = 2 * S * D_MODEL * D_CQ + 2 * S * D_CQ * 2 * HEADS * D_HEAD
 
 
-def schedule(weight):
-    waiting = [(half, part, a) for half in range(HALVES) for part in range(PARTS) for a in range(S_TILES)]
+def shares(n):
+    if n < 2:
+        return 3 * P, PIECE
+    if PIECES[n][0] == "w_cq":
+        return 2 * P, PIECE
+    return (V1 if n < C_Q_START + 4 else V2), PIECE - 1 * P if n >= C_Q_START + 7 else PIECE
+
+
+def schedule(weight, earliest):
+    waiting = [(group, a) for group in range(GROUPS) for a in range(S_TILES)]
     iterations = {}
     n = 0
     while waiting:
         iterations[n] = []
+        room = 2 if weight == "w_q" and n >= A_PAIRS_START else 1
         for step in list(waiting):
-            half, part, a = step
-            weights_ready = CQ_PIECES + W_ORDER.index((weight, half, part, PASSES_2 - 1)) + 2
-            c_q_ready = C_Q_START + C_Q_ORDER.index((PASSES_2 - 1, a)) + 3
-            room = 2 if weight == 1 and n >= A_PAIRS_START else 1
-            if n >= weights_ready and n >= c_q_ready and len(iterations[n]) < room:
+            group, a = step
+            weights_ready = max(PIECES.index((weight, group, g)) for g in range(PASSES_2)) + 2
+            c_q_ready = C_Q_ITERATION[(PASSES_2 - 1, a)] + 3
+            if n >= max(weights_ready, c_q_ready, earliest.get(step, 0)) and len(iterations[n]) < room:
                 iterations[n].append(step)
                 waiting.remove(step)
         n += 1
@@ -121,33 +114,27 @@ def tile_mla_pa_kernel(tc, h, w_cq, w_q, w_qr, out):
         ctx.enter_context(tc.manual_schedule())
         const = ctx.enter_context(tc.tile_pool(name="const", bufs=1))
         keep = ctx.enter_context(tc.tile_pool(name="keep", bufs=1))
-        cq_raw_pool = ctx.enter_context(tc.tile_pool(name="cq_raw_pool", bufs=PASSES_1))
         raw_pool = ctx.enter_context(tc.tile_pool(name="raw_pool", bufs=RAW_BUFS))
         stage = ctx.enter_context(tc.tile_pool(name="stage", bufs=4))
-        c_q_stage = ctx.enter_context(tc.tile_pool(name="c_q_stage", bufs=S_TILES))
+        c_q_stage = ctx.enter_context(tc.tile_pool(name="c_q_stage", bufs=2))
         psum_main = ctx.enter_context(tc.psum_pool(name="psum_main", bufs=PSUM_MAIN))
         psum_a = ctx.enter_context(tc.psum_pool(name="psum_a", bufs=8 - PSUM_MAIN))
 
-        w_cq_rows = w_cq.rearrange("(c p t) n -> c p t n", c=PASSES_1, t=PACK)
-        cq_raw = []
+        rows = {
+            "w_cq": w_cq.rearrange("(k p t) n -> k p t n", k=PASSES_1, t=PACK),
+            "w_qr": w_qr.rearrange("(k p t) n -> k p t n", k=PASSES_2, t=PACK),
+            "w_q": w_q.rearrange("(k p t) n -> k p t n", k=PASSES_2, t=PACK),
+        }
+        raw = {}
 
-        def load_w_cq():
-            c = len(cq_raw)
-            raw = cq_raw_pool.tile([P, PACK, D_CQ], BF16, name="cq_raw")
-            cq_raw.append(raw)
-            nc.sync.dma_start(out=raw[:], in_=w_cq_rows[c])
+        def load():
+            weight, half, k = LOADS[len(raw)]
+            tile = raw_pool.tile([P, PACK, LOAD_COLS], BF16, name="raw")
+            nc.sync.dma_start(out=tile[:], in_=rows[weight][k][:, :, half * LOAD_COLS : (half + 1) * LOAD_COLS])
+            raw[(weight, half, k)] = tile
 
         h_rows = h.flatten_outer_dims().rearrange("(p a) k -> p a k", a=S_TILES)
         h_mx = []
-        w_rows = [w.rearrange("(g p t) n -> g p t n", g=PASSES_2, t=PACK) for w in (w_qr, w_q)]
-        w_raw = {}
-
-        def load_w():
-            half, rest = divmod(len(w_raw), 2 * PASSES_2)
-            weight, g = divmod(rest, PASSES_2)
-            raw = raw_pool.tile([P, PACK, LOAD_COLS], BF16, name="w_raw")
-            nc.sync.dma_start(out=raw[:], in_=w_rows[weight][g][:, :, half * LOAD_COLS : (half + 1) * LOAD_COLS])
-            w_raw[(weight, half, g)] = raw
 
         zero = const.tile([P, 1], F32)
         nc.gpsimd.memset(zero[:], 0.0)
@@ -165,6 +152,8 @@ def tile_mla_pa_kernel(tc, h, w_cq, w_q, w_qr, out):
         )
         identity = const.tile([P, P], F32)
         make_identity(nc, identity[:])
+        identity_bf16 = const.tile([P, P], BF16)
+        nc.gpsimd.tensor_copy(out=identity_bf16[:], in_=identity[:])
         nc.vector.tensor_scalar_mul(out=position[:], in0=position[:], scalar1=1.0 / (2.0 * math.pi))
         frequency = const.tile([P, PAIRS], F32)
         nc.vector.memset(frequency[:, 0:1], 1.0)
@@ -183,19 +172,18 @@ def tile_mla_pa_kernel(tc, h, w_cq, w_q, w_qr, out):
             in1=position[:].unsqueeze(2).to_broadcast(shape),
             op=ALU.mult,
         )
-        factors = const.tile([P, 3, S_TILES, PAIRS], F32)
-        for_even = factors[:, 1:3]
-        for_odd = factors[:, 0:2]
         whole_turns = const.tile(shape, F32)
-        sin_half = const.tile(shape, F32)
-        sin_quarter = const.tile(shape, F32)
-        square = const.tile(shape, F32)
-        cos_half = const.tile(shape, F32)
-
         nc.vector.tensor_scalar(
             out=whole_turns[:], in0=turns[:], scalar1=ROUND_MAGIC, scalar2=ROUND_MAGIC, op0=ALU.add, op1=ALU.subtract
         )
         nc.vector.tensor_tensor(out=turns[:], in0=turns[:], in1=whole_turns[:], op=ALU.subtract)
+        factors = const.tile([P, 3, S_TILES, PAIRS], F32)
+        for_even = factors[:, 1:3]
+        for_odd = factors[:, 0:2]
+        sin_half = const.tile(shape, F32)
+        sin_quarter = const.tile(shape, F32)
+        square = const.tile(shape, F32)
+        cos_half = const.tile(shape, F32)
 
         def rope_sines():
             nc.scalar.activation(out=sin_half[:], in_=turns[:], func=ACT.Sin, scale=math.pi)
@@ -211,62 +199,82 @@ def tile_mla_pa_kernel(tc, h, w_cq, w_q, w_qr, out):
                     out=factors[:, plane], in0=sin_half[:], scalar=factor, in1=cos_half[:], op0=ALU.mult, op1=ALU.mult
                 )
 
-        pieces = []
-        w_cq_mx = {}
-        w_mx = {}
+        weight_mx = {}
+        grouped_pieces = {}
 
-
-        def raw_columns(n, first, last):
-            if n < CQ_PIECES:
-                g, c = CQ_ORDER[n]
-                piece = cq_raw[c][:, :, g * PIECE : (g + 1) * PIECE]
-                by_group = piece.rearrange("p j (m t) -> p j t m", t=PACK)
+        def raw_columns(piece, first, last):
+            weight, q, k = piece
+            start = q % PARTS * PIECE
+            tile = raw[(weight, q // PARTS, k)]
+            if weight == "w_cq":
+                by_group = tile[:, :, start : start + PIECE].rearrange("p j (m t) -> p j t m", t=PACK)
                 return by_group[:, :, first // P : last // P]
-            weight, half, part, g = W_ORDER[n - CQ_PIECES]
-            start = part * PIECE
-            return w_raw[(weight, half, g)][:, :, start + first : start + last]
+            return tile[:, :, start + first : start + last]
+
+        passed = {}
+
+        def pass_through(n):
+            piece = PIECES[n]
+            first = shares(n)[1]
+            if first == PIECE:
+                return
+            bank = psum_main.tile([P, PIECE - first, PACK], BF16, tag="bank", name="passed")
+            for start in range(first, PIECE, P):
+                run = raw_columns(piece, start, start + P)
+                nc.tensor.matmul(
+                    bank[:, start - first : start - first + P].rearrange("p c j -> p j c"),
+                    lhsT=identity_bf16[:],
+                    rhs=run[:, :, 0] if piece[0] == "w_cq" else run,
+                    start=True,
+                    stop=True,
+                )
+            passed[piece] = bank
 
         def regroup(n):
+            piece = PIECES[n]
             grouped = stage.tile([P, PIECE, PACK], BF16, align_bytes=64, name="grouped")
-            split = vector_columns(n)
-            for copy, first, last in ((nc.vector.tensor_copy, 0, split), (nc.scalar.copy, split, PIECE)):
-                dst, src = grouped[:, first:last], raw_columns(n, first, last)
-                if n < CQ_PIECES:
+            by_vector, by_scalar = shares(n)
+            for copy, first, last in ((nc.vector.tensor_copy, 0, by_vector), (nc.scalar.copy, by_vector, by_scalar)):
+                dst, src = grouped[:, first:last], raw_columns(piece, first, last)
+                if piece[0] == "w_cq":
                     dst = dst.rearrange("p (t m) j -> p m j t", m=P)
                     src = src.rearrange("p j t m -> p m j t")
                 else:
                     dst = dst.rearrange("p (w i) j -> p w j i", i=4)
                     src = src.rearrange("p j (w i) -> p w j i", i=4)
                 copy(out=dst, in_=src)
-            if n < CQ_PIECES:
-                operand = mx_operand(keep, PIECE, "w_cq%d" % n)
-                w_cq_mx[CQ_ORDER[n]] = operand
-            else:
-                weight, half, part, g = W_ORDER[n - CQ_PIECES]
-                operand = mx_operand(keep, PIECE, "w%d%d%d%d" % (weight, half, part, g))
-                w_mx[(weight, half, part, g)] = operand
-            pieces.append((grouped, operand))
+            if by_scalar < PIECE:
+                nc.scalar.copy(
+                    out=grouped[:, by_scalar:].rearrange("p c j -> p (c j)").bitcast(F32),
+                    in_=passed[piece][:].rearrange("p c j -> p (c j)").bitcast(F32),
+                )
+            grouped_pieces[piece] = grouped
+            weight_mx[piece] = mx_operand(keep, PIECE, "%s%d%d" % piece)
+            if piece[1] % PARTS == PARTS - 1 and len(raw) < len(LOADS):
+                load()
 
         def quantise_piece(n):
-            grouped, operand = pieces[n]
-            quantise(nc, operand, grouped[:].rearrange("p w t -> p (w t)"))
+            piece = PIECES[n]
+            quantise(nc, weight_mx[piece], grouped_pieces[piece][:].rearrange("p w t -> p (w t)"))
 
         with tc.tile_pool(name="h_pool", bufs=S_TILES) as h_pool, tc.tile_pool(name="h_stage", bufs=S_TILES) as h_stage:
-            load_w_cq()
+            while len(raw) < H_LOAD:
+                load()
             h_raw = []
             for a in range(S_TILES):
                 h_tile = h_pool.tile([P, D_MODEL], BF16)
                 nc.sync.dma_start(out=h_tile[:], in_=h_rows[:, a, :])
                 h_raw.append(h_tile)
-            while len(cq_raw) < PASSES_1:
-                load_w_cq()
-            for j in range(RAW_BUFS):
-                load_w()
+            while len(raw) < RAW_BUFS:
+                load()
 
-            regroup(0)
-            regroup(1)
-            rope_sines()
-            quantise_piece(0)
+            for n in range(BEFORE_H):
+                pass_through(n)
+                regroup(n)
+                if n == 1:
+                    rope_sines()
+                if n > 0:
+                    quantise_piece(n - 1)
             h_grouped = []
             for a in range(S_TILES):
                 h_words = h_raw[a][:].bitcast(F32)
@@ -278,61 +286,60 @@ def tile_mla_pa_kernel(tc, h, w_cq, w_q, w_qr, out):
                         c, u = divmod(4 * b + j, 2)
                         words = h_words[:, 2 * P * c + u : 2 * P * (c + 1) : 2]
                         nc.tensor.transpose(flipped[:, j, :], words, identity[:])
-                    target = grouped_a[:, 2 * b : 2 * b + 2].bitcast(F32)
-                    flipped_words = flipped[:].rearrange("q (c u) s -> q c s u", u=2)
-                    nc.scalar.copy(out=target, in_=flipped_words)
+                    nc.scalar.copy(
+                        out=grouped_a[:, 2 * b : 2 * b + 2].bitcast(F32),
+                        in_=flipped[:].rearrange("q (c u) s -> q c s u", u=2),
+                    )
                 h_mx.append(mx_operand(keep, PASSES_1 * P, "h%d" % a))
                 if a == 0:
-                    quantise_piece(1)
+                    quantise_piece(BEFORE_H - 1)
                     rope_factors()
                 else:
                     quantise(nc, h_mx[a - 1], h_grouped[a - 1][:].rearrange("q c s t -> q (c s t)"))
+            regroup(BEFORE_H)
             quantise(nc, h_mx[-1], h_grouped[-1][:].rearrange("q c s t -> q (c s t)"))
+            quantise_piece(BEFORE_H)
         rope_pool = ctx.enter_context(tc.tile_pool(name="rope_pool", bufs=3, reuse_waits="tile"))
         result_pool = ctx.enter_context(tc.tile_pool(name="result_pool", bufs=5, reuse_waits="tile"))
 
+        c_q_banks = {}
         c_q_grouped = {}
         c_q_mx = {}
         results = {}
         out_rows = out.rearrange("b n (p a) d -> p (b n) a d", a=S_TILES)
 
-        def c_q_bank(b):
-            g, a = C_Q_ORDER[b]
+        def make_c_q(g, a):
             bank = psum_main.tile([P, PACK, P], F32, tag="bank", name="c_q")
             for t in range(PACK):
                 for c in range(PASSES_1):
                     multiply_mx(
                         nc,
                         bank[:, t, :],
-                        columns(w_cq_mx[(g, c)], t * P, P),
+                        columns(weight_mx[("w_cq", g, c)], t * P, P),
                         columns(h_mx[a], c * P, P),
                         first=(c == 0),
                         last=(c == PASSES_1 - 1),
                     )
-            return bank
+            c_q_banks[(g, a)] = bank
 
-        def copy_c_q_bank(b, bank):
-            g, a = C_Q_ORDER[b]
+        def copy_c_q(g, a):
             if g == 0:
                 c_q_grouped[a] = c_q_stage.tile([P, PASSES_2, P, PACK], BF16, align_bytes=64, name="c_q_grouped")
-            nc.scalar.copy(out=c_q_grouped[a][:, g], in_=bank[:].rearrange("m t s -> m s t"))
+            nc.scalar.copy(out=c_q_grouped[a][:, g], in_=c_q_banks[(g, a)][:].rearrange("m t s -> m s t"))
 
         def quantise_c_q(a):
             c_q_mx[a] = mx_operand(keep, PASSES_2 * P, "c_q%d" % a)
             quantise(nc, c_q_mx[a], c_q_grouped[a][:].rearrange("m g s t -> m (g s t)"))
 
-        def multiply_by_weights(step, weight):
-            half, part, a = step
-            if weight == 0:
-                bank = psum_main.tile([P, GROUP_HEADS, D_HEAD], F32, tag="bank", name="u")
-            else:
-                bank = psum_a.tile([P, GROUP_HEADS, D_HEAD], F32, name="a")
+        def multiply_by_weights(step, weight, pool, tag):
+            group, a = step
+            bank = pool.tile([P, GROUP_HEADS, D_HEAD], F32, tag=tag, name=weight)
             for g in range(PASSES_2):
                 multiply_mx(
                     nc,
                     bank[:].rearrange("p n d -> p (n d)"),
                     columns(c_q_mx[a], g * P, P),
-                    columns(w_mx[(weight, half, part, g)], 0, PIECE),
+                    columns(weight_mx[(weight, group, g)], 0, PIECE),
                     first=(g == 0),
                     last=(g == PASSES_2 - 1),
                 )
@@ -354,50 +361,43 @@ def tile_mla_pa_kernel(tc, h, w_cq, w_q, w_qr, out):
             return both
 
         def result_of(step):
-            half, part, a = step
-            key = (half, part, a // STORE_TILES)
+            group, a = step
+            key = (group, a // STORE_TILES)
             if key not in results:
                 results[key] = result_pool.tile([P, GROUP_HEADS, STORE_TILES, 2 * D_HEAD], F32, name="result")
             return results[key][:, :, a % STORE_TILES]
 
-        def rope_sum(engine, step, both):
-            engine.tensor_tensor(out=result_of(step)[:, :, D_HEAD:], in0=both[0], in1=both[1], op=ALU.add)
+        def store(step):
+            group, a = step
+            heads = slice(group * GROUP_HEADS, (group + 1) * GROUP_HEADS)
+            nc.sync.dma_start(out=out_rows[:, heads, a + 1 - STORE_TILES : a + 1, :], in_=results[(group, a // STORE_TILES)][:])
 
-        def store(step, tiles):
-            half, part, a = step
-            first_head = (half * PARTS + part) * GROUP_HEADS
-            last = a % STORE_TILES + 1
-            nc.sync.dma_start(
-                out=out_rows[:, first_head : first_head + GROUP_HEADS, a + 1 - tiles : a + 1, :],
-                in_=results[(half, part, a // STORE_TILES)][:, :, last - tiles : last],
-            )
-
-        c_q_banks = {}
-        u_schedule, a_schedule = schedule(0), schedule(1)
+        u_schedule = schedule("w_qr", {})
+        a_schedule = schedule("w_q", {step: n for n in u_schedule for step in u_schedule[n]})
         last_iteration = max(a_schedule)
-        for n in range(2, last_iteration + 1):
-            b = n - C_Q_START
+        for n in range(BEFORE_H + 1, last_iteration + 1):
             u_steps, a_steps = u_schedule.get(n, []), a_schedule.get(n, [])
-            u_banks = [multiply_by_weights(step, 0) for step in u_steps]
-            a_banks = [multiply_by_weights(step, 1) for step in a_steps]
-            if n < CQ_PIECES + W_PIECES:
+            u_banks = [multiply_by_weights(step, "w_qr", psum_main, "bank") for step in u_steps]
+            a_banks = [multiply_by_weights(step, "w_q", psum_a, "a") for step in a_steps]
+            if n + 1 < len(PIECES):
+                pass_through(n + 1)
+            if n < len(PIECES):
                 regroup(n)
-                if n >= CQ_PIECES and W_ORDER[n - CQ_PIECES][2] == PARTS - 1 and len(w_raw) < W_PIECES // PARTS:
-                    load_w()
-            if 2 < n <= CQ_PIECES + W_PIECES:
+            if BEFORE_H + 1 < n <= len(PIECES):
                 quantise_piece(n - 1)
-            if 0 <= b < C_Q_BANKS:
-                c_q_banks[b] = c_q_bank(b)
-            if 1 <= b <= C_Q_BANKS:
-                copy_c_q_bank(b - 1, c_q_banks[b - 1])
-            if 2 <= b <= C_Q_BANKS + 1 and C_Q_ORDER[b - 2][0] == PASSES_2 - 1:
-                quantise_c_q(C_Q_ORDER[b - 2][1])
+            for g, a in C_Q_BANKS:
+                made = C_Q_ITERATION[(g, a)]
+                if made == n:
+                    make_c_q(g, a)
+                if made == n - 1:
+                    copy_c_q(g, a)
+                if made == n - 2 and g == PASSES_2 - 1:
+                    quantise_c_q(a)
             for step, bank in zip(u_steps, u_banks):
+                both = rope_products(step[1], bank)
                 engine = nc.vector if n == last_iteration else nc.gpsimd
-                rope_sum(engine, step, rope_products(step[2], bank))
+                engine.tensor_tensor(out=result_of(step)[:, :, D_HEAD:], in0=both[0], in1=both[1], op=ALU.add)
             for step, bank in zip(a_steps, a_banks):
                 nc.scalar.copy(out=result_of(step)[:, :, 0:D_HEAD], in_=bank[:])
-                if n == last_iteration:
-                    store(step, 1)
-                elif step[2] % STORE_TILES == STORE_TILES - 1:
-                    store(step, STORE_TILES)
+                if step[1] % STORE_TILES == STORE_TILES - 1:
+                    store(step)

@@ -36,17 +36,16 @@ GROUPS = HEADS // GROUP_HEADS
 LOADS = [("w_cq", 0, k) for k in range(PASSES_1)] + [
     (weight, half, g) for half in range(2) for weight in ("w_qr", "w_q") for g in range(PASSES_2)
 ]
-H_LOAD = PASSES_1 - 1
-PIECES = [("w_cq", q, k) for k in range(PASSES_1) for q in range(PASSES_2)] + [
+H_LOAD = PASSES_1
+PIECES = [("w_cq", q, k) for k in range(PASSES_1) for q in range(PASSES_2)] + [None, None] + [
     (weight, q, g) for weight in ("w_qr", "w_q") for q in (0, 1) for g in range(PASSES_2)
 ] + [(weight, q, g) for q in (2, 3) for weight in ("w_qr", "w_q") for g in range(PASSES_2)]
-BEFORE_H = H_LOAD * PARTS
+BEFORE_H = H_LOAD * PARTS - 2
 C_Q_BANKS = [(g, a) for a in range(S_TILES) for g in range(PASSES_2)]
 
-C_Q_START = PIECES.index(("w_cq", 0, PASSES_1 - 1)) + 1
-C_Q_ITERATION = {bank: C_Q_START + i - (i >= 2) for i, bank in enumerate(C_Q_BANKS)}
+C_Q_START = BEFORE_H + 1
+C_Q_ITERATION = {bank: C_Q_START + 1 + i for i, bank in enumerate(C_Q_BANKS)}
 A_PAIRS_START = PIECES.index(("w_q", 2, 1)) + 2
-V1, V2 = 256, 144
 RAW_BUFS = 9
 STORE_TILES = 2
 PSUM_MAIN = 6
@@ -60,8 +59,8 @@ def shares(n):
     if n < 2:
         return 3 * P, PIECE
     if PIECES[n][0] == "w_cq":
-        return 2 * P, PIECE
-    return (V1 if n < C_Q_START + 4 else V2), PIECE - 1 * P if n >= C_Q_START + 7 else PIECE
+        return 3 * P if n >= BEFORE_H else 2 * P, PIECE
+    return (256 if n < 13 else 144), PIECE - 1 * P if n >= 16 else PIECE
 
 
 def schedule(weight, earliest):
@@ -181,23 +180,18 @@ def tile_mla_pa_kernel(tc, h, w_cq, w_q, w_qr, out):
         for_even = factors[:, 1:3]
         for_odd = factors[:, 0:2]
         sin_half = const.tile(shape, F32)
-        sin_quarter = const.tile(shape, F32)
         square = const.tile(shape, F32)
-        cos_half = const.tile(shape, F32)
 
         def rope_sines():
             nc.scalar.activation(out=sin_half[:], in_=turns[:], func=ACT.Sin, scale=math.pi)
-            nc.scalar.activation(out=sin_quarter[:], in_=turns[:], func=ACT.Sin, scale=math.pi / 2.0)
+            nc.scalar.activation(out=factors[:, 2], in_=turns[:], func=ACT.Sin, scale=2.0 * math.pi)
+            nc.scalar.activation(out=factors[:, 0], in_=turns[:], func=ACT.Sin, scale=-2.0 * math.pi)
             nc.scalar.activation(out=square[:], in_=sin_half[:], func=ACT.Square)
-            nc.scalar.activation(out=cos_half[:], in_=sin_quarter[:], func=ACT.Square)
 
         def rope_factors():
-            for squared, cosine in ((square[:], factors[:, 1]), (cos_half[:], cos_half[:])):
-                nc.vector.tensor_scalar(out=cosine, in0=squared, scalar1=-2.0, scalar2=1.0, op0=ALU.mult, op1=ALU.add)
-            for factor, plane in ((2.0, 2), (-2.0, 0)):
-                nc.vector.scalar_tensor_tensor(
-                    out=factors[:, plane], in0=sin_half[:], scalar=factor, in1=cos_half[:], op0=ALU.mult, op1=ALU.mult
-                )
+            nc.vector.tensor_scalar(
+                out=factors[:, 1], in0=square[:], scalar1=-2.0, scalar2=1.0, op0=ALU.mult, op1=ALU.add
+            )
 
         weight_mx = {}
         grouped_pieces = {}
@@ -240,8 +234,8 @@ def tile_mla_pa_kernel(tc, h, w_cq, w_q, w_qr, out):
                     dst = dst.rearrange("p (t m) j -> p m j t", m=P)
                     src = src.rearrange("p j t m -> p m j t")
                 else:
-                    dst = dst.rearrange("p (w i) j -> p w j i", i=4)
-                    src = src.rearrange("p j (w i) -> p w j i", i=4)
+                    dst = dst.rearrange("p (w i) j -> p w j i", i=8)
+                    src = src.rearrange("p j (w i) -> p w j i", i=8)
                 copy(out=dst, in_=src)
             if by_scalar < PIECE:
                 nc.scalar.copy(
@@ -257,56 +251,10 @@ def tile_mla_pa_kernel(tc, h, w_cq, w_q, w_qr, out):
             piece = PIECES[n]
             quantise(nc, weight_mx[piece], grouped_pieces[piece][:].rearrange("p w t -> p (w t)"))
 
-        with tc.tile_pool(name="h_pool", bufs=S_TILES) as h_pool, tc.tile_pool(name="h_stage", bufs=S_TILES) as h_stage:
-            while len(raw) < H_LOAD:
-                load()
-            h_raw = []
-            for a in range(S_TILES):
-                h_tile = h_pool.tile([P, D_MODEL], BF16)
-                nc.sync.dma_start(out=h_tile[:], in_=h_rows[:, a, :])
-                h_raw.append(h_tile)
-            while len(raw) < RAW_BUFS:
-                load()
-
-            for n in range(BEFORE_H):
-                pass_through(n)
-                regroup(n)
-                if n == 1:
-                    rope_sines()
-                if n > 0:
-                    quantise_piece(n - 1)
-            h_grouped = []
-            for a in range(S_TILES):
-                h_words = h_raw[a][:].bitcast(F32)
-                grouped_a = h_stage.tile([P, PASSES_1, P, PACK], BF16, align_bytes=64)
-                h_grouped.append(grouped_a)
-                for b in range(PASSES_1 // 2):
-                    flipped = psum_main.tile([P, 4, P], F32, tag="bank")
-                    for j in range(4):
-                        c, u = divmod(4 * b + j, 2)
-                        words = h_words[:, 2 * P * c + u : 2 * P * (c + 1) : 2]
-                        nc.tensor.transpose(flipped[:, j, :], words, identity[:])
-                    nc.scalar.copy(
-                        out=grouped_a[:, 2 * b : 2 * b + 2].bitcast(F32),
-                        in_=flipped[:].rearrange("q (c u) s -> q c s u", u=2),
-                    )
-                h_mx.append(mx_operand(keep, PASSES_1 * P, "h%d" % a))
-                if a == 0:
-                    quantise_piece(BEFORE_H - 1)
-                    rope_factors()
-                else:
-                    quantise(nc, h_mx[a - 1], h_grouped[a - 1][:].rearrange("q c s t -> q (c s t)"))
-            regroup(BEFORE_H)
-            quantise(nc, h_mx[-1], h_grouped[-1][:].rearrange("q c s t -> q (c s t)"))
-            quantise_piece(BEFORE_H)
-        rope_pool = ctx.enter_context(tc.tile_pool(name="rope_pool", bufs=3, reuse_waits="tile"))
-        result_pool = ctx.enter_context(tc.tile_pool(name="result_pool", bufs=5, reuse_waits="tile"))
-
+        h_grouped = []
         c_q_banks = {}
         c_q_grouped = {}
         c_q_mx = {}
-        results = {}
-        out_rows = out.rearrange("b n (p a) d -> p (b n) a d", a=S_TILES)
 
         def make_c_q(g, a):
             bank = psum_main.tile([P, PACK, P], F32, tag="bank", name="c_q")
@@ -330,6 +278,78 @@ def tile_mla_pa_kernel(tc, h, w_cq, w_q, w_qr, out):
         def quantise_c_q(a):
             c_q_mx[a] = mx_operand(keep, PASSES_2 * P, "c_q%d" % a)
             quantise(nc, c_q_mx[a], c_q_grouped[a][:].rearrange("m g s t -> m (g s t)"))
+
+        def c_q_work(n):
+            for g, a in C_Q_BANKS:
+                made = C_Q_ITERATION[(g, a)]
+                if made == n:
+                    make_c_q(g, a)
+                if made == n - 1:
+                    copy_c_q(g, a)
+                if made == n - 2 and g == PASSES_2 - 1:
+                    quantise_c_q(a)
+
+        with tc.tile_pool(name="h_pool", bufs=S_TILES) as h_pool, tc.tile_pool(name="h_stage", bufs=S_TILES) as h_stage:
+            while len(raw) < H_LOAD:
+                load()
+            h_raw = []
+            for a in range(S_TILES):
+                h_tile = h_pool.tile([P, D_MODEL], BF16)
+                nc.sync.dma_start(out=h_tile[:], in_=h_rows[:, a, :])
+                h_raw.append(h_tile)
+            while len(raw) < RAW_BUFS:
+                load()
+
+            for n in range(BEFORE_H):
+                pass_through(n)
+                regroup(n)
+                if n == 1:
+                    rope_sines()
+                if n > 0:
+                    quantise_piece(n - 1)
+            def turn_h(a):
+                h_words = h_raw[a][:].bitcast(F32)
+                banks = []
+                for b in range(PASSES_1 // 2):
+                    flipped = psum_main.tile([P, 4, P], F32, tag="bank", name="flipped")
+                    for j in range(4):
+                        c, u = divmod(4 * b + j, 2)
+                        words = h_words[:, 2 * P * c + u : 2 * P * (c + 1) : 2]
+                        nc.tensor.transpose(flipped[:, j, :], words, identity[:])
+                    banks.append(flipped)
+                return banks
+
+            turned = [turn_h(0)]
+            for a in range(S_TILES):
+                n = BEFORE_H + a
+                if a + 1 < S_TILES:
+                    turned.append(turn_h(a + 1))
+                banks = turned[a]
+                if PIECES[n]:
+                    regroup(n)
+                grouped_a = h_stage.tile([P, PASSES_1, P, PACK], BF16, align_bytes=64, name="h_grouped")
+                for b, flipped in enumerate(banks):
+                    copy_h = nc.vector.tensor_copy if False else nc.scalar.copy
+                    copy_h(
+                        out=grouped_a[:, 2 * b : 2 * b + 2].bitcast(F32),
+                        in_=flipped[:].rearrange("q (c u) s -> q c s u", u=2),
+                    )
+                if PIECES[n - 1]:
+                    quantise_piece(n - 1)
+                if a == 0:
+                    rope_factors()
+                else:
+                    h_mx.append(mx_operand(keep, PASSES_1 * P, "h%d" % (a - 1)))
+                    quantise(nc, h_mx[a - 1], h_grouped[a - 1][:].rearrange("q c s t -> q (c s t)"))
+                h_grouped.append(grouped_a)
+                c_q_work(n)
+            h_mx.append(mx_operand(keep, PASSES_1 * P, "h%d" % (S_TILES - 1)))
+            quantise(nc, h_mx[-1], h_grouped[-1][:].rearrange("q c s t -> q (c s t)"))
+        rope_pool = ctx.enter_context(tc.tile_pool(name="rope_pool", bufs=3, reuse_waits="tile"))
+        result_pool = ctx.enter_context(tc.tile_pool(name="result_pool", bufs=5, reuse_waits="tile"))
+
+        results = {}
+        out_rows = out.rearrange("b n (p a) d -> p (b n) a d", a=S_TILES)
 
         def multiply_by_weights(step, weight, pool, tag):
             group, a = step
@@ -375,7 +395,7 @@ def tile_mla_pa_kernel(tc, h, w_cq, w_q, w_qr, out):
         u_schedule = schedule("w_qr", {})
         a_schedule = schedule("w_q", {step: n for n in u_schedule for step in u_schedule[n]})
         last_iteration = max(a_schedule)
-        for n in range(BEFORE_H + 1, last_iteration + 1):
+        for n in range(BEFORE_H + S_TILES, last_iteration + 1):
             u_steps, a_steps = u_schedule.get(n, []), a_schedule.get(n, [])
             u_banks = [multiply_by_weights(step, "w_qr", psum_main, "bank") for step in u_steps]
             a_banks = [multiply_by_weights(step, "w_q", psum_a, "a") for step in a_steps]
@@ -383,16 +403,9 @@ def tile_mla_pa_kernel(tc, h, w_cq, w_q, w_qr, out):
                 pass_through(n + 1)
             if n < len(PIECES):
                 regroup(n)
-            if BEFORE_H + 1 < n <= len(PIECES):
+            if BEFORE_H + S_TILES < n <= len(PIECES):
                 quantise_piece(n - 1)
-            for g, a in C_Q_BANKS:
-                made = C_Q_ITERATION[(g, a)]
-                if made == n:
-                    make_c_q(g, a)
-                if made == n - 1:
-                    copy_c_q(g, a)
-                if made == n - 2 and g == PASSES_2 - 1:
-                    quantise_c_q(a)
+            c_q_work(n)
             for step, bank in zip(u_steps, u_banks):
                 both = rope_products(step[1], bank)
                 engine = nc.vector if n == last_iteration else nc.gpsimd

import math
from contextlib import ExitStack

import concourse.mybir as mybir
from concourse.masks import make_identity

F32 = mybir.dt.float32
BF16 = mybir.dt.bfloat16
U32 = mybir.dt.uint32
U8 = mybir.dt.uint8
FP8X4 = mybir.dt.float8_e4m3fn_x4
ALU = mybir.AluOpType
ACT = mybir.ActivationFunctionType

P = 128
PACK = 4
K_PASS = P * PACK

S = 512
D_MODEL = 2048
D_CQ = 1024
HEADS = 16
D_HEAD = 128
PAIRS = D_HEAD // 2
ROPE_BASE = 10000.0

S_TILES = S // P
PASSES_1 = D_MODEL // K_PASS
PASSES_2 = D_CQ // K_PASS
PIECE = 512
PARTS = 2
LOAD_COLS = PARTS * PIECE
GROUP_HEADS = PIECE // D_HEAD
GROUPS = HEADS // GROUP_HEADS

LOADS = [("w_cq", 0, k) for k in range(PASSES_1)] + [
    (weight, half, g) for half in range(2) for weight in ("w_qr", "w_q") for g in range(PASSES_2)
]
H_LOAD = PASSES_1
PIECES = [("w_cq", q, k) for k in range(PASSES_1) for q in range(PASSES_2)] + [None, None] + [
    (weight, q, g) for weight in ("w_qr", "w_q") for q in (0, 1) for g in range(PASSES_2)
] + [(weight, q, g) for q in (2, 3) for weight in ("w_qr", "w_q") for g in range(PASSES_2)]
BEFORE_H = H_LOAD * PARTS - 2
C_Q_BANKS = [(g, a) for a in range(S_TILES) for g in range(PASSES_2)]

C_Q_START = BEFORE_H + 1
C_Q_ITERATION = {bank: C_Q_START + 1 + i for i, bank in enumerate(C_Q_BANKS)}
A_PAIRS_START = PIECES.index(("w_q", 2, 1)) + 2
RAW_BUFS = 9
STORE_TILES = 2
PSUM_MAIN = 6

ROUND_MAGIC = 1.5 * 2.0**23

FLOPS = 2 * S * D_MODEL * D_CQ + 2 * S * D_CQ * 2 * HEADS * D_HEAD


def shares(n):
    if n < 2:
        return 3 * P, PIECE
    if PIECES[n][0] == "w_cq":
        return 3 * P if n >= BEFORE_H else 2 * P, PIECE
    return (256 if n < 13 else 144), PIECE - 1 * P if n >= 16 else PIECE


def schedule(weight, earliest):
    waiting = [(group, a) for group in range(GROUPS) for a in range(S_TILES)]
    iterations = {}
    n = 0
    while waiting:
        iterations[n] = []
        room = 2 if weight == "w_q" and n >= A_PAIRS_START else 1
        for step in list(waiting):
            group, a = step
            weights_ready = max(PIECES.index((weight, group, g)) for g in range(PASSES_2)) + 2
            c_q_ready = C_Q_ITERATION[(PASSES_2 - 1, a)] + 3
            if n >= max(weights_ready, c_q_ready, earliest.get(step, 0)) and len(iterations[n]) < room:
                iterations[n].append(step)
                waiting.remove(step)
        n += 1
    return iterations


def quantise(nc, operand, grouped):
    nc.vector.quantize_mx(out=operand[0][:].bitcast(FP8X4), scales=operand[1][:], in_=grouped)


def mx_operand(pool, width, label):
    codes = pool.tile([P, width], U32, align_bytes=64, name=label + "_codes")
    scales = pool.tile([P, width], U8, align_bytes=64, name=label + "_scales")
    return codes, scales


def columns(operand, start, width):
    return operand[0][:, start : start + width], operand[1][:, start : start + width]


def multiply_mx(nc, acc, stationary, moving, first, last):
    nc.tensor.matmul_mx(
        out=acc,
        lhsT=stationary[0].bitcast(FP8X4),
        lhsT_scale=stationary[1],
        rhs=moving[0].bitcast(FP8X4),
        rhs_scale=moving[1],
        start=first,
        stop=last,
    )


def tile_mla_pa_kernel(tc, h, w_cq, w_q, w_qr, out):
    nc = tc.nc
    with ExitStack() as ctx:
        ctx.enter_context(tc.manual_schedule())
        const = ctx.enter_context(tc.tile_pool(name="const", bufs=1))
        keep = ctx.enter_context(tc.tile_pool(name="keep", bufs=1))
        raw_pool = ctx.enter_context(tc.tile_pool(name="raw_pool", bufs=RAW_BUFS))
        stage = ctx.enter_context(tc.tile_pool(name="stage", bufs=4))
        c_q_stage = ctx.enter_context(tc.tile_pool(name="c_q_stage", bufs=2))
        psum_main = ctx.enter_context(tc.psum_pool(name="psum_main", bufs=PSUM_MAIN))
        psum_a = ctx.enter_context(tc.psum_pool(name="psum_a", bufs=8 - PSUM_MAIN))

        rows = {
            "w_cq": w_cq.rearrange("(k p t) n -> k p t n", k=PASSES_1, t=PACK),
            "w_qr": w_qr.rearrange("(k p t) n -> k p t n", k=PASSES_2, t=PACK),
            "w_q": w_q.rearrange("(k p t) n -> k p t n", k=PASSES_2, t=PACK),
        }
        raw = {}

        def load():
            weight, half, k = LOADS[len(raw)]
            tile = raw_pool.tile([P, PACK, LOAD_COLS], BF16, name="raw")
            nc.sync.dma_start(out=tile[:], in_=rows[weight][k][:, :, half * LOAD_COLS : (half + 1) * LOAD_COLS])
            raw[(weight, half, k)] = tile

        h_rows = h.flatten_outer_dims().rearrange("(p a) k -> p a k", a=S_TILES)
        h_mx = []

        zero = const.tile([P, 1], F32)
        nc.gpsimd.memset(zero[:], 0.0)
        sin_zero = const.tile([P, 1], F32)
        nc.scalar.activation(out=sin_zero[:], in_=zero[:], func=ACT.Sin)

        shape = [P, S_TILES, PAIRS]
        position = const.tile([P, S_TILES], F32)
        nc.gpsimd.iota(
            position[:],
            pattern=[[1, S_TILES]],
            base=0,
            channel_multiplier=S_TILES,
            allow_small_or_imprecise_dtypes=True,
        )
        identity = const.tile([P, P], F32)
        make_identity(nc, identity[:])
        identity_bf16 = const.tile([P, P], BF16)
        nc.gpsimd.tensor_copy(out=identity_bf16[:], in_=identity[:])
        nc.vector.tensor_scalar_mul(out=position[:], in0=position[:], scalar1=1.0 / (2.0 * math.pi))
        frequency = const.tile([P, PAIRS], F32)
        nc.vector.memset(frequency[:, 0:1], 1.0)
        filled = 1
        while filled < PAIRS:
            nc.vector.tensor_scalar_mul(
                out=frequency[:, filled : 2 * filled],
                in0=frequency[:, 0:filled],
                scalar1=ROPE_BASE ** (-2.0 * filled / D_HEAD),
            )
            filled *= 2
        turns = const.tile(shape, F32)
        nc.vector.tensor_tensor(
            out=turns[:],
            in0=frequency[:].unsqueeze(1).to_broadcast(shape),
            in1=position[:].unsqueeze(2).to_broadcast(shape),
            op=ALU.mult,
        )
        whole_turns = const.tile(shape, F32)
        nc.vector.tensor_scalar(
            out=whole_turns[:], in0=turns[:], scalar1=ROUND_MAGIC, scalar2=ROUND_MAGIC, op0=ALU.add, op1=ALU.subtract
        )
        nc.vector.tensor_tensor(out=turns[:], in0=turns[:], in1=whole_turns[:], op=ALU.subtract)
        factors = const.tile([P, 3, S_TILES, PAIRS], F32)
        for_even = factors[:, 1:3]
        for_odd = factors[:, 0:2]
        sin_half = const.tile(shape, F32)
        square = const.tile(shape, F32)

        def rope_sines():
            nc.scalar.activation(out=sin_half[:], in_=turns[:], func=ACT.Sin, scale=math.pi)
            nc.scalar.activation(out=factors[:, 2], in_=turns[:], func=ACT.Sin, scale=2.0 * math.pi)
            nc.scalar.activation(out=factors[:, 0], in_=turns[:], func=ACT.Sin, scale=-2.0 * math.pi)
            nc.scalar.activation(out=square[:], in_=sin_half[:], func=ACT.Square)

        def rope_factors():
            nc.vector.tensor_scalar(
                out=factors[:, 1], in0=square[:], scalar1=-2.0, scalar2=1.0, op0=ALU.mult, op1=ALU.add
            )

        weight_mx = {}
        grouped_pieces = {}

        def raw_columns(piece, first, last):
            weight, q, k = piece
            start = q % PARTS * PIECE
            tile = raw[(weight, q // PARTS, k)]
            if weight == "w_cq":
                by_group = tile[:, :, start : start + PIECE].rearrange("p j (m t) -> p j t m", t=PACK)
                return by_group[:, :, first // P : last // P]
            return tile[:, :, start + first : start + last]

        passed = {}

        def pass_through(n):
            piece = PIECES[n]
            first = shares(n)[1]
            if first == PIECE:
                return
            bank = psum_main.tile([P, PIECE - first, PACK], BF16, tag="bank", name="passed")
            for start in range(first, PIECE, P):
                run = raw_columns(piece, start, start + P)
                nc.tensor.matmul(
                    bank[:, start - first : start - first + P].rearrange("p c j -> p j c"),
                    lhsT=identity_bf16[:],
                    rhs=run[:, :, 0] if piece[0] == "w_cq" else run,
                    start=True,
                    stop=True,
                )
            passed[piece] = bank

        def regroup(n):
            piece = PIECES[n]
            grouped = stage.tile([P, PIECE, PACK], BF16, align_bytes=64, name="grouped")
            by_vector, by_scalar = shares(n)
            for copy, first, last in ((nc.vector.tensor_copy, 0, by_vector), (nc.scalar.copy, by_vector, by_scalar)):
                dst, src = grouped[:, first:last], raw_columns(piece, first, last)
                if piece[0] == "w_cq":
                    dst = dst.rearrange("p (t m) j -> p m j t", m=P)
                    src = src.rearrange("p j t m -> p m j t")
                else:
                    dst = dst.rearrange("p (w i) j -> p w j i", i=8)
                    src = src.rearrange("p j (w i) -> p w j i", i=8)
                copy(out=dst, in_=src)
            if by_scalar < PIECE:
                nc.scalar.copy(
                    out=grouped[:, by_scalar:].rearrange("p c j -> p (c j)").bitcast(F32),
                    in_=passed[piece][:].rearrange("p c j -> p (c j)").bitcast(F32),
                )
            grouped_pieces[piece] = grouped
            weight_mx[piece] = mx_operand(keep, PIECE, "%s%d%d" % piece)
            if piece[1] % PARTS == PARTS - 1 and len(raw) < len(LOADS):
                load()

        def quantise_piece(n):
            piece = PIECES[n]
            quantise(nc, weight_mx[piece], grouped_pieces[piece][:].rearrange("p w t -> p (w t)"))

        h_grouped = []
        c_q_banks = {}
        c_q_grouped = {}
        c_q_mx = {}

        def make_c_q(g, a):
            bank = psum_main.tile([P, PACK, P], F32, tag="bank", name="c_q")
            for t in range(PACK):
                for c in range(PASSES_1):
                    multiply_mx(
                        nc,
                        bank[:, t, :],
                        columns(weight_mx[("w_cq", g, c)], t * P, P),
                        columns(h_mx[a], c * P, P),
                        first=(c == 0),
                        last=(c == PASSES_1 - 1),
                    )
            c_q_banks[(g, a)] = bank

        def copy_c_q(g, a):
            if g == 0:
                c_q_grouped[a] = c_q_stage.tile([P, PASSES_2, P, PACK], BF16, align_bytes=64, name="c_q_grouped")
            nc.scalar.copy(out=c_q_grouped[a][:, g], in_=c_q_banks[(g, a)][:].rearrange("m t s -> m s t"))

        def quantise_c_q(a):
            c_q_mx[a] = mx_operand(keep, PASSES_2 * P, "c_q%d" % a)
            quantise(nc, c_q_mx[a], c_q_grouped[a][:].rearrange("m g s t -> m (g s t)"))

        def c_q_work(n):
            for g, a in C_Q_BANKS:
                made = C_Q_ITERATION[(g, a)]
                if made == n:
                    make_c_q(g, a)
                if made == n - 1:
                    copy_c_q(g, a)
                if made == n - 2 and g == PASSES_2 - 1:
                    quantise_c_q(a)

        with tc.tile_pool(name="h_pool", bufs=S_TILES) as h_pool, tc.tile_pool(name="h_stage", bufs=S_TILES) as h_stage:
            while len(raw) < H_LOAD:
                load()
            h_raw = []
            for a in range(S_TILES):
                h_tile = h_pool.tile([P, D_MODEL], BF16)
                nc.sync.dma_start(out=h_tile[:], in_=h_rows[:, a, :])
                h_raw.append(h_tile)
            while len(raw) < RAW_BUFS:
                load()

            for n in range(BEFORE_H):
                pass_through(n)
                regroup(n)
                if n == 1:
                    rope_sines()
                if n > 0:
                    quantise_piece(n - 1)
            def turn_h(a):
                h_words = h_raw[a][:].bitcast(F32)
                banks = []
                for b in range(PASSES_1 // 2):
                    flipped = psum_main.tile([P, 4, P], F32, tag="bank", name="flipped")
                    for j in range(4):
                        c, u = divmod(4 * b + j, 2)
                        words = h_words[:, 2 * P * c + u : 2 * P * (c + 1) : 2]
                        nc.tensor.transpose(flipped[:, j, :], words, identity[:])
                    banks.append(flipped)
                return banks

            turned = [turn_h(0)]
            for a in range(S_TILES):
                n = BEFORE_H + a
                if a + 1 < S_TILES:
                    turned.append(turn_h(a + 1))
                banks = turned[a]
                if PIECES[n]:
                    regroup(n)
                grouped_a = h_stage.tile([P, PASSES_1, P, PACK], BF16, align_bytes=64, name="h_grouped")
                for b, flipped in enumerate(banks):
                    copy_h = nc.vector.tensor_copy if False else nc.scalar.copy
                    copy_h(
                        out=grouped_a[:, 2 * b : 2 * b + 2].bitcast(F32),
                        in_=flipped[:].rearrange("q (c u) s -> q c s u", u=2),
                    )
                if PIECES[n - 1]:
                    quantise_piece(n - 1)
                if a == 0:
                    rope_factors()
                else:
                    h_mx.append(mx_operand(keep, PASSES_1 * P, "h%d" % (a - 1)))
                    quantise(nc, h_mx[a - 1], h_grouped[a - 1][:].rearrange("q c s t -> q (c s t)"))
                h_grouped.append(grouped_a)
                c_q_work(n)
            h_mx.append(mx_operand(keep, PASSES_1 * P, "h%d" % (S_TILES - 1)))
            quantise(nc, h_mx[-1], h_grouped[-1][:].rearrange("q c s t -> q (c s t)"))
        rope_pool = ctx.enter_context(tc.tile_pool(name="rope_pool", bufs=3, reuse_waits="tile"))
        result_pool = ctx.enter_context(tc.tile_pool(name="result_pool", bufs=5, reuse_waits="tile"))

        results = {}
        out_rows = out.rearrange("b n (p a) d -> p (b n) a d", a=S_TILES)

        def multiply_by_weights(step, weight, pool, tag):
            group, a = step
            bank = pool.tile([P, GROUP_HEADS, D_HEAD], F32, tag=tag, name=weight)
            for g in range(PASSES_2):
                multiply_mx(
                    nc,
                    bank[:].rearrange("p n d -> p (n d)"),
                    columns(c_q_mx[a], g * P, P),
                    columns(weight_mx[(weight, group, g)], 0, PIECE),
                    first=(g == 0),
                    last=(g == PASSES_2 - 1),
                )
            return bank

        def rope_products(a, u_bank):
            whole = [P, GROUP_HEADS, PAIRS, 2]
            u_pairs = u_bank[:].rearrange("p n (i e) -> p n i e", e=2)
            both = []
            for e, pair in ((0, for_even), (1, for_odd)):
                product = rope_pool.tile(whole, F32, name="product%d" % e)
                nc.vector.tensor_tensor(
                    out=product[:],
                    in0=u_pairs[:, :, :, e : e + 1].to_broadcast(whole),
                    in1=pair[:, :, a].rearrange("p e i -> p i e").unsqueeze(1).to_broadcast(whole),
                    op=ALU.mult,
                )
                both.append(product[:].rearrange("p n i e -> p n (i e)"))
            return both

        def result_of(step):
            group, a = step
            key = (group, a // STORE_TILES)
            if key not in results:
                results[key] = result_pool.tile([P, GROUP_HEADS, STORE_TILES, 2 * D_HEAD], F32, name="result")
            return results[key][:, :, a % STORE_TILES]

        def store(step):
            group, a = step
            heads = slice(group * GROUP_HEADS, (group + 1) * GROUP_HEADS)
            nc.sync.dma_start(out=out_rows[:, heads, a + 1 - STORE_TILES : a + 1, :], in_=results[(group, a // STORE_TILES)][:])

        u_schedule = schedule("w_qr", {})
        a_schedule = schedule("w_q", {step: n for n in u_schedule for step in u_schedule[n]})
        last_iteration = max(a_schedule)
        for n in range(BEFORE_H + S_TILES, last_iteration + 1):
            u_steps, a_steps = u_schedule.get(n, []), a_schedule.get(n, [])
            u_banks = [multiply_by_weights(step, "w_qr", psum_main, "bank") for step in u_steps]
            a_banks = [multiply_by_weights(step, "w_q", psum_a, "a") for step in a_steps]
            if n + 1 < len(PIECES):
                pass_through(n + 1)
            if n < len(PIECES):
                regroup(n)
            if BEFORE_H + S_TILES < n <= len(PIECES):
                quantise_piece(n - 1)
            c_q_work(n)
            for step, bank in zip(u_steps, u_banks):
                both = rope_products(step[1], bank)
                engine = nc.vector if n == last_iteration else nc.gpsimd
                engine.tensor_tensor(out=result_of(step)[:, :, D_HEAD:], in0=both[0], in1=both[1], op=ALU.add)
            for step, bank in zip(a_steps, a_banks):
                nc.scalar.copy(out=result_of(step)[:, :, 0:D_HEAD], in_=bank[:])
                if step[1] % STORE_TILES == STORE_TILES - 1:
                    store(step)
